import numpy as np
import ml_dtypes


def mxq(x, axis, fmt="e4m3"):
    dtype, down = {"e4m3": (ml_dtypes.float8_e4m3fn, 7), "e5m2": (ml_dtypes.float8_e5m2, 14)}[fmt]
    v = np.moveaxis(np.asarray(x, np.float32).astype(ml_dtypes.bfloat16).astype(np.float64), axis, -1)
    blocks = v.reshape(v.shape[:-1] + (-1, 32))
    amax = np.abs(blocks).max(-1, keepdims=True)
    byte = np.maximum(np.where(amax > 0, np.frexp(amax)[1] - 1 + 127, 0) - down, 1)
    scale = np.exp2(byte - 127.0)
    codes = (blocks / scale).astype(np.float32).astype(dtype).astype(np.float64)
    return np.moveaxis((codes * scale).reshape(v.shape), -1, axis)


WIDE = False


def mx_kscale(k):
    if not WIDE:
        return np.ones(k)
    levels = np.array([10, -10, 5, -5, 0])
    a = np.random.permutation(np.resize(levels, k // 512 * 4)).reshape(k // 512, 4)
    idx = np.arange(k)
    return np.exp2(a[idx // 512, idx % 128 // 32])


BF16 = ml_dtypes.bfloat16


def bf(x):
    return np.asarray(x, np.float32).astype(BF16)


def f64(x):
    return np.asarray(x).astype(np.float64)


B, N, F, D = 3, 512, 128, 128


def normalize_adjacency(adj):
    d = np.sum(adj, axis=-1)
    with np.errstate(divide="ignore"):
        d_sqrt_inv = np.power(d, -0.5)
    d_sqrt_inv = np.where(np.isinf(d_sqrt_inv), 0.0, d_sqrt_inv)
    return d_sqrt_inv[..., :, None] * adj * d_sqrt_inv[..., None, :]


def setup_inputs():
    s = mx_kscale(N)
    g = s.mean()
    a = np.exp2(np.random.uniform(-2.0, 2.0, size=(B, N, 1)))
    return {"inputs": bf(np.random.standard_normal((B, N, F)) * (g / s)[:, None]),
            "adj": bf(np.random.uniform(size=(B, N, N)) * a * s),
            "W_kernel": bf(np.random.standard_normal((F, D)) * 0.2 * np.sqrt(N / F)),
            "W_bias": bf(np.random.standard_normal(D) * 0.2)}


def reference(inputs, adj, W_kernel, W_bias):
    adj_norm = normalize_adjacency(f64(adj))
    feats = f64(inputs) @ f64(W_kernel) + f64(W_bias)
    out = mxq(adj_norm, 2, "e4m3") @ mxq(feats, 1, "e4m3")
    return np.maximum(out, 0.0)

@@ -1,0 +1,156 @@
+from contextlib import ExitStack
+
+import concourse.mybir as mybir
+from concourse.masks import make_identity
+
+BF16 = mybir.dt.bfloat16
+F32 = mybir.dt.float32
+U32 = mybir.dt.uint32
+U8 = mybir.dt.uint8
+FP8X4 = mybir.dt.float8_e4m3fn_x4
+ALU = mybir.AluOpType
+FUNC = mybir.ActivationFunctionType
+
+GRAPHS = 3
+NODES = 512
+FEATS = 128
+DIM = 128
+P = 128
+PACK = 4
+TINY = 1e-30
+
+FLOPS = 2 * GRAPHS * NODES * (NODES * DIM + FEATS * DIM)
+
+
+def tile_gcn_s_kernel(tc, inputs, adj, W_kernel, W_bias, out):
+    nc = tc.nc
+    with ExitStack() as stack:
+        const = stack.enter_context(tc.tile_pool(name="const", bufs=1))
+        loads = stack.enter_context(tc.tile_pool(name="loads", bufs=GRAPHS))
+        small = stack.enter_context(tc.tile_pool(name="small", bufs=GRAPHS))
+        work = stack.enter_context(tc.tile_pool(name="work", bufs=2))
+        psum = stack.enter_context(tc.psum_pool(name="psum", bufs=1))
+
+        w_sb = const.tile([FEATS, DIM], BF16)
+        bias_row = const.tile([P, DIM], BF16)
+        nc.vector.memset(bias_row[:], 0.0)
+        adj_tiles = []
+        x_tiles = []
+        for b in range(GRAPHS):
+            adj_sb = loads.tile([P, PACK, NODES], BF16)
+            adj_rows = adj[b].rearrange("(p t) m -> t p m", t=PACK)
+            for t in range(PACK):
+                nc.sync.dma_start(out=adj_sb[:, t, :], in_=adj_rows[t])
+            adj_tiles.append(adj_sb)
+            if b == 0:
+                nc.sync.dma_start(out=w_sb[:], in_=W_kernel)
+                nc.sync.dma_start(out=bias_row[0:1, :], in_=W_bias.rearrange("(o d) -> o d", o=1))
+            x_sb = loads.tile([P, PACK, FEATS], BF16)
+            nc.sync.dma_start(out=x_sb[:], in_=inputs[b].rearrange("(p t) f -> p t f", t=PACK))
+            x_tiles.append(x_sb)
+
+        one = const.tile([P, 1], F32)
+        nc.vector.memset(one[:], 1.0)
+        warm = const.tile([P, 1], F32)
+        nc.scalar.activation(out=warm[:], in_=one[:], func=FUNC.Sqrt)
+        ident_bf = const.tile([P, P], BF16)
+        make_identity(nc, ident_bf[:])
+        ident_f32 = const.tile([P, P], F32)
+        make_identity(nc, ident_f32[:])
+        ones = const.tile([P, P], BF16)
+        nc.vector.memset(ones[:], 1.0)
+        bias_ps = psum.tile([P, DIM], F32, tag="feats")
+        nc.tensor.matmul(out=bias_ps[:], lhsT=ones[:], rhs=bias_row[:], start=True, stop=True)
+        bias_all = const.tile([P, DIM], F32)
+        nc.vector.tensor_copy(out=bias_all[:], in_=bias_ps[:])
+
+        for b in range(GRAPHS):
+            adj_sb = adj_tiles[b]
+            x_sb = x_tiles[b]
+
+            xT_ps = psum.tile([FEATS, PACK, P], BF16, tag="xT")
+            for t in range(PACK):
+                nc.tensor.transpose(xT_ps[:, t, :], x_sb[:, t, :], ident_bf[:])
+            xT_sb = work.tile([FEATS, PACK, P], BF16)
+            nc.vector.tensor_copy(out=xT_sb[:], in_=xT_ps[:])
+            feats_ps = psum.tile([P, PACK, DIM], F32, tag="feats")
+            for t in range(PACK):
+                nc.tensor.matmul(
+                    out=feats_ps[:, t, :], lhsT=xT_sb[:, t, :], rhs=w_sb[:], start=True, stop=True
+                )
+            feats_grouped = work.tile([P, DIM, PACK], BF16, align_bytes=64)
+            nc.vector.tensor_tensor(
+                out=feats_grouped[:],
+                in0=feats_ps[:].rearrange("p t d -> p d t"),
+                in1=bias_all[:].unsqueeze(2).to_broadcast([P, DIM, PACK]),
+                op=ALU.add,
+            )
+            feats_codes = work.tile([P, DIM], U32, align_bytes=64)
+            feats_scales = work.tile([P, DIM], U8, align_bytes=64)
+            nc.vector.quantize_mx(
+                out=feats_codes[:].bitcast(FP8X4),
+                scales=feats_scales[:],
+                in_=feats_grouped[:].rearrange("p d t -> p (d t)"),
+            )
+
+            degree = small.tile([P, PACK], F32)
+            for t in range(PACK):
+                unused = work.tile([P, NODES], BF16)
+                nc.scalar.activation(
+                    out=unused[:], in_=adj_sb[:, t, :], func=FUNC.Copy,
+                    accum_out=degree[:, t : t + 1],
+                )
+            root = small.tile([P, PACK], F32)
+            nc.scalar.activation(out=root[:], in_=degree[:], func=FUNC.Sqrt)
+            safe_root = small.tile([P, PACK], F32)
+            nc.vector.tensor_scalar_max(out=safe_root[:], in0=root[:], scalar1=TINY)
+            inverse = small.tile([P, PACK], F32)
+            nc.vector.reciprocal(out=inverse[:], in_=safe_root[:])
+            r = small.tile([P, PACK], F32)
+            nc.vector.scalar_tensor_tensor(
+                out=r[:], in0=degree[:], scalar=0.0, in1=inverse[:], op0=ALU.is_gt, op1=ALU.mult
+            )
+
+            norm_grouped = work.tile([P, PACK, P, PACK], BF16, align_bytes=64)
+            for t in range(PACK):
+                scaled = work.tile([P, PACK, P], F32, bufs=4)
+                nc.gpsimd.tensor_scalar(
+                    out=scaled[:],
+                    in0=adj_sb[:, t, :].rearrange("p (c j) -> p j c", j=PACK),
+                    scalar1=r[:, t : t + 1],
+                    scalar2=0.0,
+                    op0=ALU.mult,
+                    op1=ALU.add,
+                )
+                normT_ps = psum.tile([P, PACK, P], F32, tag="normT", bufs=4)
+                for j in range(PACK):
+                    nc.tensor.transpose(normT_ps[:, j, :], scaled[:, j, :], ident_f32[:])
+                nc.vector.tensor_tensor(
+                    out=norm_grouped[:, t, :, :],
+                    in0=normT_ps[:].rearrange("c j n -> c n j"),
+                    in1=r[:].unsqueeze(1).to_broadcast([P, P, PACK]),
+                    op=ALU.mult,
+                )
+            norm_codes = work.tile([P, PACK * P], U32, align_bytes=64)
+            norm_scales = work.tile([P, PACK * P], U8, align_bytes=64)
+            nc.vector.quantize_mx(
+                out=norm_codes[:].bitcast(FP8X4),
+                scales=norm_scales[:],
+                in_=norm_grouped[:].rearrange("c t n j -> c (t n j)"),
+            )
+
+            out_ps = psum.tile([P, PACK, DIM], F32, tag="out", bufs=2)
+            for t in range(PACK):
+                rows = slice(t * P, (t + 1) * P)
+                nc.tensor.matmul_mx(
+                    out=out_ps[:, t, :],
+                    lhsT=norm_codes[:, rows].bitcast(FP8X4),
+                    lhsT_scale=norm_scales[:, rows],
+                    rhs=feats_codes[:].bitcast(FP8X4),
+                    rhs_scale=feats_scales[:],
+                    start=True,
+                    stop=True,
+                )
+            out_sb = work.tile([P, PACK, DIM], F32)
+            nc.scalar.activation(out=out_sb[:], in_=out_ps[:], func=FUNC.Relu)
+            nc.sync.dma_start(out=out[b].rearrange("(p t) d -> p t d", t=PACK), in_=out_sb[:])

@@ -17,140 +17,220 @@ FEATS = 128
 DIM = 128
 P = 128
 PACK = 4
-TINY = 1e-30
+HUGE = 3.0e38
 
 FLOPS = 2 * GRAPHS * NODES * (NODES * DIM + FEATS * DIM)
+
+UNITS = GRAPHS * PACK
+HALF = 2
+LAG = 4
+BLOCK = 8
 
 
 def tile_gcn_s_kernel(tc, inputs, adj, W_kernel, W_bias, out):
     nc = tc.nc
     with ExitStack() as stack:
         const = stack.enter_context(tc.tile_pool(name="const", bufs=1))
-        loads = stack.enter_context(tc.tile_pool(name="loads", bufs=GRAPHS))
-        small = stack.enter_context(tc.tile_pool(name="small", bufs=GRAPHS))
+        graph = stack.enter_context(tc.tile_pool(name="graph", bufs=GRAPHS))
         work = stack.enter_context(tc.tile_pool(name="work", bufs=2))
         psum = stack.enter_context(tc.psum_pool(name="psum", bufs=1))
 
         w_sb = const.tile([FEATS, DIM], BF16)
         bias_row = const.tile([P, DIM], BF16)
-        nc.vector.memset(bias_row[:], 0.0)
+        x_sb = const.tile([P, GRAPHS, PACK, FEATS], BF16)
+        nc.gpsimd.memset(bias_row[:], 0.0)
         adj_tiles = []
-        x_tiles = []
         for b in range(GRAPHS):
-            adj_sb = loads.tile([P, PACK, NODES], BF16)
+            adj_sb = graph.tile([P, PACK, NODES], BF16)
+            adj_tiles.append(adj_sb)
             adj_rows = adj[b].rearrange("(p t) m -> t p m", t=PACK)
             for t in range(PACK):
                 nc.sync.dma_start(out=adj_sb[:, t, :], in_=adj_rows[t])
-            adj_tiles.append(adj_sb)
             if b == 0:
                 nc.sync.dma_start(out=w_sb[:], in_=W_kernel)
-                nc.sync.dma_start(out=bias_row[0:1, :], in_=W_bias.rearrange("(o d) -> o d", o=1))
-            x_sb = loads.tile([P, PACK, FEATS], BF16)
-            nc.sync.dma_start(out=x_sb[:], in_=inputs[b].rearrange("(p t) f -> p t f", t=PACK))
-            x_tiles.append(x_sb)
+                nc.sync.dma_start(
+                    out=bias_row[0:1, :], in_=W_bias.rearrange("(o d) -> o d", o=1)
+                )
+                nc.sync.dma_start(
+                    out=x_sb[:], in_=inputs.rearrange("b (p t) f -> p b t f", t=PACK)
+                )
 
         one = const.tile([P, 1], F32)
         nc.vector.memset(one[:], 1.0)
         warm = const.tile([P, 1], F32)
         nc.scalar.activation(out=warm[:], in_=one[:], func=FUNC.Sqrt)
+        ones = const.tile([P, P], BF16)
+        nc.gpsimd.memset(ones[:], 1.0)
         ident_bf = const.tile([P, P], BF16)
         make_identity(nc, ident_bf[:])
         ident_f32 = const.tile([P, P], F32)
         make_identity(nc, ident_f32[:])
-        ones = const.tile([P, P], BF16)
-        nc.vector.memset(ones[:], 1.0)
-        bias_ps = psum.tile([P, DIM], F32, tag="feats")
-        nc.tensor.matmul(out=bias_ps[:], lhsT=ones[:], rhs=bias_row[:], start=True, stop=True)
-        bias_all = const.tile([P, DIM], F32)
-        nc.vector.tensor_copy(out=bias_all[:], in_=bias_ps[:])
 
-        for b in range(GRAPHS):
-            adj_sb = adj_tiles[b]
-            x_sb = x_tiles[b]
+        def bank(dtype):
+            return psum.tile([P, PACK, P], dtype, name="bank", tag="bank", bufs=6)
 
-            xT_ps = psum.tile([FEATS, PACK, P], BF16, tag="xT")
+        degree_views = []
+        r_tiles = []
+
+        def sum_rows(b):
+            degree = graph.tile([P, 2, BLOCK], F32)
+            degree_views.append(degree[:, :, 0 : PACK // 2].rearrange("p e i -> p i e"))
             for t in range(PACK):
-                nc.tensor.transpose(xT_ps[:, t, :], x_sb[:, t, :], ident_bf[:])
-            xT_sb = work.tile([FEATS, PACK, P], BF16)
+                rows = adj_tiles[b][:, t, :]
+                total = degree[:, t % 2, t // 2 : t // 2 + 1]
+                if b == 0 and t % 2 == 1:
+                    nc.vector.reduce_sum(out=total, in_=rows, axis=mybir.AxisListType.X)
+                else:
+                    unused = work.tile([P, NODES], BF16)
+                    nc.scalar.activation(
+                        out=unused[:], in_=rows, func=FUNC.Copy, accum_out=total
+                    )
+
+        def inverse_root(b):
+            degree = degree_views[b]
+            pairs = "p (i e) -> p i e"
+            positive = graph.tile([P, PACK], F32)
+            nc.vector.tensor_single_scalar(
+                out=positive[:].rearrange(pairs, e=2), in_=degree, scalar=0.0, op=ALU.is_gt
+            )
+            root = graph.tile([P, PACK], F32)
+            nc.scalar.activation(out=root[:].rearrange(pairs, e=2), in_=degree, func=FUNC.Sqrt)
+            inverse = graph.tile([P, PACK], F32)
+            nc.vector.reciprocal(out=inverse[:], in_=root[:])
+            r = graph.tile([P, PACK], F32)
+            nc.vector.scalar_tensor_tensor(
+                out=r[:], in0=inverse[:], scalar=HUGE, in1=positive[:], op0=ALU.min, op1=ALU.mult
+            )
+            r_tiles.append(r)
+
+        sum_rows(0)
+        inverse_root(0)
+
+        bias_ps = bank(F32)
+        nc.tensor.matmul(
+            out=bias_ps[:, 0, :], lhsT=ones[:], rhs=bias_row[:], start=True, stop=True
+        )
+        bias_all = const.tile([P, DIM], F32)
+        nc.vector.tensor_copy(out=bias_all[:], in_=bias_ps[:, 0, :])
+        xT_tiles = []
+        for b in range(GRAPHS):
+            xT_ps = bank(BF16)
+            for t in range(PACK):
+                nc.tensor.transpose(xT_ps[:, t, :], x_sb[:, b, t, :], ident_bf[:])
+            xT_sb = graph.tile([FEATS, PACK, P], BF16)
             nc.vector.tensor_copy(out=xT_sb[:], in_=xT_ps[:])
-            feats_ps = psum.tile([P, PACK, DIM], F32, tag="feats")
+            xT_tiles.append(xT_sb)
+        feats_banks = []
+        for b in range(GRAPHS):
+            feats_ps = bank(F32)
             for t in range(PACK):
                 nc.tensor.matmul(
-                    out=feats_ps[:, t, :], lhsT=xT_sb[:, t, :], rhs=w_sb[:], start=True, stop=True
+                    out=feats_ps[:, t, :], lhsT=xT_tiles[b][:, t, :], rhs=w_sb[:],
+                    start=True, stop=True,
                 )
-            feats_grouped = work.tile([P, DIM, PACK], BF16, align_bytes=64)
+            feats_banks.append(feats_ps)
+        feats_tiles = []
+        for b in range(GRAPHS):
+            feats_grouped = graph.tile([P, DIM, PACK], BF16, align_bytes=64)
             nc.vector.tensor_tensor(
                 out=feats_grouped[:],
-                in0=feats_ps[:].rearrange("p t d -> p d t"),
+                in0=feats_banks[b][:].rearrange("p t d -> p d t"),
                 in1=bias_all[:].unsqueeze(2).to_broadcast([P, DIM, PACK]),
                 op=ALU.add,
             )
-            feats_codes = work.tile([P, DIM], U32, align_bytes=64)
-            feats_scales = work.tile([P, DIM], U8, align_bytes=64)
+            feats_codes = graph.tile([P, DIM], U32, align_bytes=64)
+            feats_scales = graph.tile([P, DIM], U8, align_bytes=64)
             nc.vector.quantize_mx(
                 out=feats_codes[:].bitcast(FP8X4),
                 scales=feats_scales[:],
                 in_=feats_grouped[:].rearrange("p d t -> p (d t)"),
             )
+            feats_tiles.append((feats_codes, feats_scales))
+        sum_rows(1)
 
-            degree = small.tile([P, PACK], F32)
-            for t in range(PACK):
-                unused = work.tile([P, NODES], BF16)
-                nc.scalar.activation(
-                    out=unused[:], in_=adj_sb[:, t, :], func=FUNC.Copy,
-                    accum_out=degree[:, t : t + 1],
-                )
-            root = small.tile([P, PACK], F32)
-            nc.scalar.activation(out=root[:], in_=degree[:], func=FUNC.Sqrt)
-            safe_root = small.tile([P, PACK], F32)
-            nc.vector.tensor_scalar_max(out=safe_root[:], in0=root[:], scalar1=TINY)
-            inverse = small.tile([P, PACK], F32)
-            nc.vector.reciprocal(out=inverse[:], in_=safe_root[:])
-            r = small.tile([P, PACK], F32)
-            nc.vector.scalar_tensor_tensor(
-                out=r[:], in0=degree[:], scalar=0.0, in1=inverse[:], op0=ALU.is_gt, op1=ALU.mult
-            )
+        scaled_tiles = {}
+        grouped_tiles = []
+        codes_tiles = []
+        scales_tiles = []
 
-            norm_grouped = work.tile([P, PACK, P, PACK], BF16, align_bytes=64)
-            for t in range(PACK):
-                scaled = work.tile([P, PACK, P], F32, bufs=4)
+        def by_scalar(unit):
+            return unit // PACK == GRAPHS - 1 and unit % 2 == 1
+
+        def scale_rows(unit):
+            b, t = divmod(unit, PACK)
+            columns = adj_tiles[b][:, t, :].rearrange("p (c j) -> p j c", j=PACK)
+            factor = r_tiles[b][:, t : t + 1]
+            if by_scalar(unit):
+                scaled = work.tile([P, PACK, P], F32, name="scaled_s", bufs=2)
+                nc.scalar.activation(out=scaled[:], in_=columns, func=FUNC.Copy, scale=factor)
+            else:
+                scaled = work.tile([P, PACK, P], F32, name="scaled_g", bufs=4)
                 nc.gpsimd.tensor_scalar(
-                    out=scaled[:],
-                    in0=adj_sb[:, t, :].rearrange("p (c j) -> p j c", j=PACK),
-                    scalar1=r[:, t : t + 1],
-                    scalar2=0.0,
-                    op0=ALU.mult,
-                    op1=ALU.add,
+                    out=scaled[:], in0=columns, scalar1=factor, scalar2=0.0,
+                    op0=ALU.mult, op1=ALU.add,
                 )
-                normT_ps = psum.tile([P, PACK, P], F32, tag="normT", bufs=4)
-                for j in range(PACK):
-                    nc.tensor.transpose(normT_ps[:, j, :], scaled[:, j, :], ident_f32[:])
-                nc.vector.tensor_tensor(
-                    out=norm_grouped[:, t, :, :],
-                    in0=normT_ps[:].rearrange("c j n -> c n j"),
-                    in1=r[:].unsqueeze(1).to_broadcast([P, P, PACK]),
-                    op=ALU.mult,
-                )
-            norm_codes = work.tile([P, PACK * P], U32, align_bytes=64)
-            norm_scales = work.tile([P, PACK * P], U8, align_bytes=64)
-            nc.vector.quantize_mx(
-                out=norm_codes[:].bitcast(FP8X4),
-                scales=norm_scales[:],
-                in_=norm_grouped[:].rearrange("c t n j -> c (t n j)"),
+            scaled_tiles[unit] = scaled
+
+        def normalise(unit):
+            b, t = divmod(unit, PACK)
+            normT_ps = bank(F32)
+            for j in range(PACK):
+                nc.tensor.transpose(normT_ps[:, j, :], scaled_tiles[unit][:, j, :], ident_f32[:])
+            nc.vector.tensor_tensor(
+                out=grouped_tiles[b][:, t, :, :],
+                in0=normT_ps[:].rearrange("c j n -> c n j"),
+                in1=r_tiles[b][:].unsqueeze(1).to_broadcast([P, P, PACK]),
+                op=ALU.mult,
             )
 
-            out_ps = psum.tile([P, PACK, DIM], F32, tag="out", bufs=2)
-            for t in range(PACK):
-                rows = slice(t * P, (t + 1) * P)
+        def quantise(unit):
+            b, t = divmod(unit, PACK)
+            nc.vector.quantize_mx(
+                out=codes_tiles[b][:, t, :].bitcast(FP8X4),
+                scales=scales_tiles[b][:, t, :],
+                in_=grouped_tiles[b][:, t, :, :].rearrange("c n j -> c (n j)"),
+            )
+
+        def multiply(first_unit):
+            b, t0 = divmod(first_unit, PACK)
+            feats_codes, feats_scales = feats_tiles[b]
+            out_ps = psum.tile([P, HALF, DIM], F32, bufs=2)
+            for h in range(HALF):
                 nc.tensor.matmul_mx(
-                    out=out_ps[:, t, :],
-                    lhsT=norm_codes[:, rows].bitcast(FP8X4),
-                    lhsT_scale=norm_scales[:, rows],
+                    out=out_ps[:, h, :],
+                    lhsT=codes_tiles[b][:, t0 + h, :].bitcast(FP8X4),
+                    lhsT_scale=scales_tiles[b][:, t0 + h, :],
                     rhs=feats_codes[:].bitcast(FP8X4),
                     rhs_scale=feats_scales[:],
                     start=True,
                     stop=True,
                 )
-            out_sb = work.tile([P, PACK, DIM], F32)
+            out_sb = work.tile([P, HALF, DIM], F32)
             nc.scalar.activation(out=out_sb[:], in_=out_ps[:], func=FUNC.Relu)
-            nc.sync.dma_start(out=out[b].rearrange("(p t) d -> p t d", t=PACK), in_=out_sb[:])
+            out_rows = out[b].rearrange("(p t) d -> p t d", t=PACK)
+            nc.sync.dma_start(out=out_rows[:, t0 : t0 + HALF, :], in_=out_sb[:])
+
+        for step in range(UNITS + LAG):
+            b, t = divmod(step, PACK)
+            if step < UNITS:
+                if t == 0:
+                    norm_grouped = graph.tile([P, PACK, P, PACK], BF16, align_bytes=64)
+                    grouped_tiles.append(norm_grouped)
+                    norm_codes = graph.tile([P, PACK, P], U32, align_bytes=64)
+                    codes_tiles.append(norm_codes)
+                    norm_scales = graph.tile([P, PACK, P], U8, align_bytes=64)
+                    scales_tiles.append(norm_scales)
+                if not by_scalar(step):
+                    scale_rows(step)
+                normalise(step)
+            if t == 0 and b + 1 < GRAPHS:
+                inverse_root(b + 1)
+                if b + 2 < GRAPHS:
+                    sum_rows(b + 2)
+                for unit in range((b + 1) * PACK, (b + 2) * PACK):
+                    if by_scalar(unit):
+                        scale_rows(unit)
+            if 1 <= step <= UNITS:
+                quantise(step - 1)
+            if 0 <= step - LAG < UNITS and (step - LAG) % HALF == 0:
+                multiply(step - LAG)

@@ -183,12 +183,13 @@ def tile_gcn_s_kernel(tc, inputs, adj, W_kernel, W_bias, out):
                 op=ALU.mult,
             )
 
-        def quantise(unit):
-            b, t = divmod(unit, PACK)
+        def quantise(first_unit):
+            b, t0 = divmod(first_unit, PACK)
+            rows = slice(t0, t0 + HALF)
             nc.vector.quantize_mx(
-                out=codes_tiles[b][:, t, :].bitcast(FP8X4),
-                scales=scales_tiles[b][:, t, :],
-                in_=grouped_tiles[b][:, t, :, :].rearrange("c n j -> c (n j)"),
+                out=codes_tiles[b][:, rows, :].rearrange("c t n -> c (t n)").bitcast(FP8X4),
+                scales=scales_tiles[b][:, rows, :].rearrange("c t n -> c (t n)"),
+                in_=grouped_tiles[b][:, rows, :, :].rearrange("c t n j -> c (t n j)"),
             )
 
         def multiply(first_unit):
@@ -230,7 +231,7 @@ def tile_gcn_s_kernel(tc, inputs, adj, W_kernel, W_bias, out):
                 for unit in range((b + 1) * PACK, (b + 2) * PACK):
                     if by_scalar(unit):
                         scale_rows(unit)
-            if 1 <= step <= UNITS:
-                quantise(step - 1)
+            if HALF <= step <= UNITS and step % HALF == 0:
+                quantise(step - HALF)
             if 0 <= step - LAG < UNITS and (step - LAG) % HALF == 0:
                 multiply(step - LAG)

@@ -34,6 +34,7 @@ def tile_gcn_s_kernel(tc, inputs, adj, W_kernel, W_bias, out):
         graph = stack.enter_context(tc.tile_pool(name="graph", bufs=GRAPHS))
         work = stack.enter_context(tc.tile_pool(name="work", bufs=2))
         psum = stack.enter_context(tc.psum_pool(name="psum", bufs=1))
+        stack.enter_context(tc.manual_schedule())
 
         w_sb = const.tile([FEATS, DIM], BF16)
         bias_row = const.tile([P, DIM], BF16)
@@ -183,13 +184,12 @@ def tile_gcn_s_kernel(tc, inputs, adj, W_kernel, W_bias, out):
                 op=ALU.mult,
             )
 
-        def quantise(first_unit):
-            b, t0 = divmod(first_unit, PACK)
-            rows = slice(t0, t0 + HALF)
+        def quantise(unit):
+            b, t = divmod(unit, PACK)
             nc.vector.quantize_mx(
-                out=codes_tiles[b][:, rows, :].rearrange("c t n -> c (t n)").bitcast(FP8X4),
-                scales=scales_tiles[b][:, rows, :].rearrange("c t n -> c (t n)"),
-                in_=grouped_tiles[b][:, rows, :, :].rearrange("c t n j -> c (t n j)"),
+                out=codes_tiles[b][:, t, :].bitcast(FP8X4),
+                scales=scales_tiles[b][:, t, :],
+                in_=grouped_tiles[b][:, t, :, :].rearrange("c n j -> c (n j)"),
             )
 
         def multiply(first_unit):
@@ -231,7 +231,7 @@ def tile_gcn_s_kernel(tc, inputs, adj, W_kernel, W_bias, out):
                 for unit in range((b + 1) * PACK, (b + 2) * PACK):
                     if by_scalar(unit):
                         scale_rows(unit)
-            if HALF <= step <= UNITS and step % HALF == 0:
-                quantise(step - HALF)
+            if 1 <= step <= UNITS:
+                quantise(step - 1)
             if 0 <= step - LAG < UNITS and (step - LAG) % HALF == 0:
                 multiply(step - LAG)

@@ -206,7 +206,7 @@ def tile_gcn_s_kernel(tc, inputs, adj, W_kernel, W_bias, out):
                     start=True,
                     stop=True,
                 )
-            out_sb = work.tile([P, HALF, DIM], F32)
+            out_sb = work.tile([P, HALF, DIM], F32, name="out_sb", bufs=UNITS // HALF)
             nc.scalar.activation(out=out_sb[:], in_=out_ps[:], func=FUNC.Relu)
             out_rows = out[b].rearrange("(p t) d -> p t d", t=PACK)
             nc.sync.dma_start(out=out_rows[:, t0 : t0 + HALF, :], in_=out_sb[:])

@@ -131,7 +131,10 @@ def tile_gcn_s_kernel(tc, inputs, adj, W_kernel, W_bias, out):
                 )
             feats_banks.append(feats_ps)
         feats_tiles = []
+        sum_rows(1)
         for b in range(GRAPHS):
+            if b == GRAPHS - 1:
+                inverse_root(1)
             feats_grouped = graph.tile([P, DIM, PACK], BF16, align_bytes=64)
             nc.vector.tensor_tensor(
                 out=feats_grouped[:],
@@ -147,7 +150,7 @@ def tile_gcn_s_kernel(tc, inputs, adj, W_kernel, W_bias, out):
                 in_=feats_grouped[:].rearrange("p d t -> p (d t)"),
             )
             feats_tiles.append((feats_codes, feats_scales))
-        sum_rows(1)
+        sum_rows(2)
 
         scaled_tiles = {}
         grouped_tiles = []
@@ -224,11 +227,9 @@ def tile_gcn_s_kernel(tc, inputs, adj, W_kernel, W_bias, out):
                 if not by_scalar(step):
                     scale_rows(step)
                 normalise(step)
-            if t == 0 and b + 1 < GRAPHS:
-                inverse_root(b + 1)
-                if b + 2 < GRAPHS:
-                    sum_rows(b + 2)
-                for unit in range((b + 1) * PACK, (b + 2) * PACK):
+            if step == 0:
+                inverse_root(GRAPHS - 1)
+                for unit in range((GRAPHS - 1) * PACK, UNITS):
                     if by_scalar(unit):
                         scale_rows(unit)
             if 1 <= step <= UNITS:

@@ -158,14 +158,14 @@ def tile_gcn_s_kernel(tc, inputs, adj, W_kernel, W_bias, out):
         scales_tiles = []
 
         def by_scalar(unit):
-            return unit // PACK == GRAPHS - 1 and unit % 2 == 1
+            return unit >= PACK
 
         def scale_rows(unit):
             b, t = divmod(unit, PACK)
             columns = adj_tiles[b][:, t, :].rearrange("p (c j) -> p j c", j=PACK)
             factor = r_tiles[b][:, t : t + 1]
             if by_scalar(unit):
-                scaled = work.tile([P, PACK, P], F32, name="scaled_s", bufs=2)
+                scaled = work.tile([P, PACK, P], F32, name="scaled_s", bufs=4)
                 nc.scalar.activation(out=scaled[:], in_=columns, func=FUNC.Copy, scale=factor)
             else:
                 scaled = work.tile([P, PACK, P], F32, name="scaled_g", bufs=4)
@@ -229,9 +229,8 @@ def tile_gcn_s_kernel(tc, inputs, adj, W_kernel, W_bias, out):
                 normalise(step)
             if step == 0:
                 inverse_root(GRAPHS - 1)
-                for unit in range((GRAPHS - 1) * PACK, UNITS):
-                    if by_scalar(unit):
-                        scale_rows(unit)
+            if step + PACK < UNITS:
+                scale_rows(step + PACK)
             if 1 <= step <= UNITS:
                 quantise(step - 1)
             if 0 <= step - LAG < UNITS and (step - LAG) % HALF == 0:

@@ -23,6 +23,7 @@ FLOPS = 2 * GRAPHS * NODES * (NODES * DIM + FEATS * DIM)
 
 UNITS = GRAPHS * PACK
 HALF = 2
+BY_GPSIMD = 6
 LAG = 4
 BLOCK = 8
 
@@ -52,9 +53,10 @@ def tile_gcn_s_kernel(tc, inputs, adj, W_kernel, W_bias, out):
                 nc.sync.dma_start(
                     out=bias_row[0:1, :], in_=W_bias.rearrange("(o d) -> o d", o=1)
                 )
-                nc.sync.dma_start(
-                    out=x_sb[:], in_=inputs.rearrange("b (p t) f -> p b t f", t=PACK)
-                )
+                for g in range(GRAPHS):
+                    nc.sync.dma_start(
+                        out=x_sb[:, g, :, :], in_=inputs[g].rearrange("(p t) f -> p t f", t=PACK)
+                    )
 
         one = const.tile([P, 1], F32)
         nc.vector.memset(one[:], 1.0)
@@ -87,70 +89,75 @@ def tile_gcn_s_kernel(tc, inputs, adj, W_kernel, W_bias, out):
                         out=unused[:], in_=rows, func=FUNC.Copy, accum_out=total
                     )
 
-        def inverse_root(b):
-            degree = degree_views[b]
-            pairs = "p (i e) -> p i e"
-            positive = graph.tile([P, PACK], F32)
-            nc.vector.tensor_single_scalar(
-                out=positive[:].rearrange(pairs, e=2), in_=degree, scalar=0.0, op=ALU.is_gt
+        root_tiles = []
+        pairs = "p (i e) -> p i e"
+
+        def take_root(b):
+            root = graph.tile([P, PACK], F32, name="root")
+            nc.scalar.activation(
+                out=root[:].rearrange(pairs, e=2), in_=degree_views[b], func=FUNC.Sqrt
             )
-            root = graph.tile([P, PACK], F32)
-            nc.scalar.activation(out=root[:].rearrange(pairs, e=2), in_=degree, func=FUNC.Sqrt)
-            inverse = graph.tile([P, PACK], F32)
-            nc.vector.reciprocal(out=inverse[:], in_=root[:])
-            r = graph.tile([P, PACK], F32)
+            root_tiles.append(root)
+
+        def invert_root(b):
+            positive = graph.tile([P, PACK], F32, name="positive")
+            nc.vector.tensor_single_scalar(
+                out=positive[:].rearrange(pairs, e=2), in_=degree_views[b], scalar=0.0,
+                op=ALU.is_gt,
+            )
+            inverse = graph.tile([P, PACK], F32, name="inverse")
+            nc.vector.reciprocal(out=inverse[:], in_=root_tiles[b][:])
+            r = graph.tile([P, PACK], F32, name="r")
             nc.vector.scalar_tensor_tensor(
                 out=r[:], in0=inverse[:], scalar=HUGE, in1=positive[:], op0=ALU.min, op1=ALU.mult
             )
             r_tiles.append(r)
 
-        sum_rows(0)
-        inverse_root(0)
+        xT_banks = {}
+        xT_tiles = {}
+        feats_banks = {}
+        grouped_feats = {}
+        feats_tiles = {}
 
-        bias_ps = bank(F32)
-        nc.tensor.matmul(
-            out=bias_ps[:, 0, :], lhsT=ones[:], rhs=bias_row[:], start=True, stop=True
-        )
-        bias_all = const.tile([P, DIM], F32)
-        nc.vector.tensor_copy(out=bias_all[:], in_=bias_ps[:, 0, :])
-        xT_tiles = []
-        for b in range(GRAPHS):
+        def turn_inputs(b):
             xT_ps = bank(BF16)
             for t in range(PACK):
                 nc.tensor.transpose(xT_ps[:, t, :], x_sb[:, b, t, :], ident_bf[:])
-            xT_sb = graph.tile([FEATS, PACK, P], BF16)
-            nc.vector.tensor_copy(out=xT_sb[:], in_=xT_ps[:])
-            xT_tiles.append(xT_sb)
-        feats_banks = []
-        for b in range(GRAPHS):
+            xT_banks[b] = xT_ps
+
+        def copy_inputs(b):
+            xT_sb = graph.tile([FEATS, PACK, P], BF16, name="xT_sb")
+            nc.vector.tensor_copy(out=xT_sb[:], in_=xT_banks[b][:])
+            xT_tiles[b] = xT_sb
+
+        def make_feats(b):
             feats_ps = bank(F32)
             for t in range(PACK):
                 nc.tensor.matmul(
                     out=feats_ps[:, t, :], lhsT=xT_tiles[b][:, t, :], rhs=w_sb[:],
                     start=True, stop=True,
                 )
-            feats_banks.append(feats_ps)
-        feats_tiles = []
-        sum_rows(1)
-        for b in range(GRAPHS):
-            if b == GRAPHS - 1:
-                inverse_root(1)
-            feats_grouped = graph.tile([P, DIM, PACK], BF16, align_bytes=64)
+            feats_banks[b] = feats_ps
+
+        def add_bias(b):
+            feats_grouped = graph.tile([P, DIM, PACK], BF16, align_bytes=64, name="feats_grouped")
             nc.vector.tensor_tensor(
                 out=feats_grouped[:],
                 in0=feats_banks[b][:].rearrange("p t d -> p d t"),
                 in1=bias_all[:].unsqueeze(2).to_broadcast([P, DIM, PACK]),
                 op=ALU.add,
             )
-            feats_codes = graph.tile([P, DIM], U32, align_bytes=64)
-            feats_scales = graph.tile([P, DIM], U8, align_bytes=64)
+            grouped_feats[b] = feats_grouped
+
+        def quantise_feats(b):
+            feats_codes = graph.tile([P, DIM], U32, align_bytes=64, name="feats_codes")
+            feats_scales = graph.tile([P, DIM], U8, align_bytes=64, name="feats_scales")
             nc.vector.quantize_mx(
                 out=feats_codes[:].bitcast(FP8X4),
                 scales=feats_scales[:],
-                in_=feats_grouped[:].rearrange("p d t -> p (d t)"),
+                in_=grouped_feats[b][:].rearrange("p d t -> p (d t)"),
             )
-            feats_tiles.append((feats_codes, feats_scales))
-        sum_rows(2)
+            feats_tiles[b] = (feats_codes, feats_scales)
 
         scaled_tiles = {}
         grouped_tiles = []
@@ -158,7 +165,7 @@ def tile_gcn_s_kernel(tc, inputs, adj, W_kernel, W_bias, out):
         scales_tiles = []
 
         def by_scalar(unit):
-            return unit >= PACK
+            return unit >= BY_GPSIMD
 
         def scale_rows(unit):
             b, t = divmod(unit, PACK)
@@ -168,7 +175,7 @@ def tile_gcn_s_kernel(tc, inputs, adj, W_kernel, W_bias, out):
                 scaled = work.tile([P, PACK, P], F32, name="scaled_s", bufs=4)
                 nc.scalar.activation(out=scaled[:], in_=columns, func=FUNC.Copy, scale=factor)
             else:
-                scaled = work.tile([P, PACK, P], F32, name="scaled_g", bufs=4)
+                scaled = work.tile([P, PACK, P], F32, name="scaled_g", bufs=BY_GPSIMD)
                 nc.gpsimd.tensor_scalar(
                     out=scaled[:], in0=columns, scalar1=factor, scalar2=0.0,
                     op0=ALU.mult, op1=ALU.add,
@@ -177,6 +184,13 @@ def tile_gcn_s_kernel(tc, inputs, adj, W_kernel, W_bias, out):
 
         def normalise(unit):
             b, t = divmod(unit, PACK)
+            if t == 0:
+                norm_grouped = graph.tile([P, PACK, P, PACK], BF16, align_bytes=64)
+                grouped_tiles.append(norm_grouped)
+                norm_codes = graph.tile([P, PACK, P], U32, align_bytes=64)
+                codes_tiles.append(norm_codes)
+                norm_scales = graph.tile([P, PACK, P], U8, align_bytes=64)
+                scales_tiles.append(norm_scales)
             normT_ps = bank(F32)
             for j in range(PACK):
                 nc.tensor.transpose(normT_ps[:, j, :], scaled_tiles[unit][:, j, :], ident_f32[:])
@@ -214,24 +228,51 @@ def tile_gcn_s_kernel(tc, inputs, adj, W_kernel, W_bias, out):
             out_rows = out[b].rearrange("(p t) d -> p t d", t=PACK)
             nc.sync.dma_start(out=out_rows[:, t0 : t0 + HALF, :], in_=out_sb[:])
 
-        for step in range(UNITS + LAG):
-            b, t = divmod(step, PACK)
+        sum_rows(0)
+        bias_ps = bank(F32)
+        nc.tensor.matmul(
+            out=bias_ps[:, 0, :], lhsT=ones[:], rhs=bias_row[:], start=True, stop=True
+        )
+        bias_all = const.tile([P, DIM], F32)
+        nc.scalar.copy(out=bias_all[:], in_=bias_ps[:, 0, :])
+        turn_inputs(0)
+        copy_inputs(0)
+        take_root(0)
+        invert_root(0)
+        for unit in range(PACK):
+            scale_rows(unit)
+        turn_inputs(1)
+        make_feats(0)
+        copy_inputs(1)
+        turn_inputs(2)
+        make_feats(1)
+        sum_rows(1)
+        take_root(1)
+        add_bias(0)
+        copy_inputs(2)
+        make_feats(2)
+        add_bias(1)
+        add_bias(2)
+        invert_root(1)
+        for unit in range(PACK, BY_GPSIMD):
+            scale_rows(unit)
+        sum_rows(2)
+        take_root(2)
+        for unit in range(PACK):
+            normalise(unit)
+        for unit in range(BY_GPSIMD, 2 * PACK):
+            scale_rows(unit)
+        for b in range(GRAPHS):
+            quantise_feats(b)
+        invert_root(2)
+        for unit in range(PACK):
+            quantise(unit)
+        for step in range(PACK, UNITS + LAG):
             if step < UNITS:
-                if t == 0:
-                    norm_grouped = graph.tile([P, PACK, P, PACK], BF16, align_bytes=64)
-                    grouped_tiles.append(norm_grouped)
-                    norm_codes = graph.tile([P, PACK, P], U32, align_bytes=64)
-                    codes_tiles.append(norm_codes)
-                    norm_scales = graph.tile([P, PACK, P], U8, align_bytes=64)
-                    scales_tiles.append(norm_scales)
-                if not by_scalar(step):
-                    scale_rows(step)
                 normalise(step)
-            if step == 0:
-                inverse_root(GRAPHS - 1)
             if step + PACK < UNITS:
                 scale_rows(step + PACK)
-            if 1 <= step <= UNITS:
+            if PACK < step <= UNITS:
                 quantise(step - 1)
-            if 0 <= step - LAG < UNITS and (step - LAG) % HALF == 0:
+            if (step - LAG) % HALF == 0:
                 multiply(step - LAG)

@@ -24,6 +24,7 @@ FLOPS = 2 * GRAPHS * NODES * (NODES * DIM + FEATS * DIM)
 UNITS = GRAPHS * PACK
 HALF = 2
 BY_GPSIMD = 6
+WARM_UP = 14
 LAG = 4
 BLOCK = 8
 
@@ -201,12 +202,13 @@ def tile_gcn_s_kernel(tc, inputs, adj, W_kernel, W_bias, out):
                 op=ALU.mult,
             )
 
-        def quantise(unit):
-            b, t = divmod(unit, PACK)
+        def quantise(first_unit, count):
+            b, t0 = divmod(first_unit, PACK)
+            tiles = slice(t0, t0 + count)
             nc.vector.quantize_mx(
-                out=codes_tiles[b][:, t, :].bitcast(FP8X4),
-                scales=scales_tiles[b][:, t, :],
-                in_=grouped_tiles[b][:, t, :, :].rearrange("c n j -> c (n j)"),
+                out=codes_tiles[b][:, tiles, :].rearrange("c t n -> c (t n)").bitcast(FP8X4),
+                scales=scales_tiles[b][:, tiles, :].rearrange("c t n -> c (t n)"),
+                in_=grouped_tiles[b][:, tiles, :, :].rearrange("c t n j -> c (t n j)"),
             )
 
         def multiply(first_unit):
@@ -228,6 +230,9 @@ def tile_gcn_s_kernel(tc, inputs, adj, W_kernel, W_bias, out):
             out_rows = out[b].rearrange("(p t) d -> p t d", t=PACK)
             nc.sync.dma_start(out=out_rows[:, t0 : t0 + HALF, :], in_=out_sb[:])
 
+        idle_ps = bank(BF16)
+        for i in range(WARM_UP):
+            nc.tensor.transpose(idle_ps[:, i % PACK, :], ident_bf[:], ident_bf[:])
         sum_rows(0)
         bias_ps = bank(F32)
         nc.tensor.matmul(
@@ -265,14 +270,16 @@ def tile_gcn_s_kernel(tc, inputs, adj, W_kernel, W_bias, out):
         for b in range(GRAPHS):
             quantise_feats(b)
         invert_root(2)
-        for unit in range(PACK):
-            quantise(unit)
+        quantise(0, PACK)
         for step in range(PACK, UNITS + LAG):
             if step < UNITS:
                 normalise(step)
             if step + PACK < UNITS:
                 scale_rows(step + PACK)
-            if PACK < step <= UNITS:
-                quantise(step - 1)
-            if (step - LAG) % HALF == 0:
-                multiply(step - LAG)
+            if PACK + HALF <= step < UNITS and step % HALF == 0:
+                quantise(step - HALF, HALF)
+            if UNITS - 1 <= step <= UNITS:
+                quantise(step - 1, 1)
+            for i in range(UNITS // HALF):
+                if step == max(HALF * i + LAG, i + 6):
+                    multiply(HALF * i)

@@ -25,7 +25,6 @@ UNITS = GRAPHS * PACK
 HALF = 2
 BY_GPSIMD = 6
 WARM_UP = 14
-LAG = 4
 BLOCK = 8
 
 
@@ -46,9 +45,10 @@ def tile_gcn_s_kernel(tc, inputs, adj, W_kernel, W_bias, out):
         for b in range(GRAPHS):
             adj_sb = graph.tile([P, PACK, NODES], BF16)
             adj_tiles.append(adj_sb)
-            adj_rows = adj[b].rearrange("(p t) m -> t p m", t=PACK)
-            for t in range(PACK):
-                nc.sync.dma_start(out=adj_sb[:, t, :], in_=adj_rows[t])
+            adj_rows = adj[b].rearrange("(p t) m -> p t m", t=PACK)
+            size = 1 if b == 0 else HALF
+            for t in range(0, PACK, size):
+                nc.sync.dma_start(out=adj_sb[:, t : t + size, :], in_=adj_rows[:, t : t + size, :])
             if b == 0:
                 nc.sync.dma_start(out=w_sb[:], in_=W_kernel)
                 nc.sync.dma_start(
@@ -211,11 +211,11 @@ def tile_gcn_s_kernel(tc, inputs, adj, W_kernel, W_bias, out):
                 in_=grouped_tiles[b][:, tiles, :, :].rearrange("c t n j -> c (t n j)"),
             )
 
-        def multiply(first_unit):
+        def multiply(first_unit, count, by_vector):
             b, t0 = divmod(first_unit, PACK)
             feats_codes, feats_scales = feats_tiles[b]
-            out_ps = psum.tile([P, HALF, DIM], F32, bufs=2)
-            for h in range(HALF):
+            out_ps = psum.tile([P, PACK, DIM], F32, name="out_ps", bufs=2)
+            for h in range(count):
                 nc.tensor.matmul_mx(
                     out=out_ps[:, h, :],
                     lhsT=codes_tiles[b][:, t0 + h, :].bitcast(FP8X4),
@@ -225,10 +225,17 @@ def tile_gcn_s_kernel(tc, inputs, adj, W_kernel, W_bias, out):
                     start=True,
                     stop=True,
                 )
-            out_sb = work.tile([P, HALF, DIM], F32, name="out_sb", bufs=UNITS // HALF)
-            nc.scalar.activation(out=out_sb[:], in_=out_ps[:], func=FUNC.Relu)
+            out_sb = work.tile([P, PACK, DIM], F32, name="out_sb", bufs=5)
+            if by_vector:
+                nc.vector.tensor_scalar_max(
+                    out=out_sb[:, 0:count, :], in0=out_ps[:, 0:count, :], scalar1=0.0
+                )
+            else:
+                nc.scalar.activation(
+                    out=out_sb[:, 0:count, :], in_=out_ps[:, 0:count, :], func=FUNC.Relu
+                )
             out_rows = out[b].rearrange("(p t) d -> p t d", t=PACK)
-            nc.sync.dma_start(out=out_rows[:, t0 : t0 + HALF, :], in_=out_sb[:])
+            nc.sync.dma_start(out=out_rows[:, t0 : t0 + count, :], in_=out_sb[:, 0:count, :])
 
         idle_ps = bank(BF16)
         for i in range(WARM_UP):
@@ -258,12 +265,13 @@ def tile_gcn_s_kernel(tc, inputs, adj, W_kernel, W_bias, out):
         make_feats(2)
         add_bias(1)
         add_bias(2)
+        normalise(0)
         invert_root(1)
         for unit in range(PACK, BY_GPSIMD):
             scale_rows(unit)
         sum_rows(2)
         take_root(2)
-        for unit in range(PACK):
+        for unit in range(1, PACK):
             normalise(unit)
         for unit in range(BY_GPSIMD, 2 * PACK):
             scale_rows(unit)
@@ -271,15 +279,17 @@ def tile_gcn_s_kernel(tc, inputs, adj, W_kernel, W_bias, out):
             quantise_feats(b)
         invert_root(2)
         quantise(0, PACK)
-        for step in range(PACK, UNITS + LAG):
+        for step in range(PACK, UNITS + 1):
             if step < UNITS:
                 normalise(step)
             if step + PACK < UNITS:
                 scale_rows(step + PACK)
             if PACK + HALF <= step < UNITS and step % HALF == 0:
                 quantise(step - HALF, HALF)
+            if step in (PACK + 3, 2 * PACK + 2):
+                multiply((step // PACK - 1) * PACK, PACK, False)
+            if step == UNITS - 1:
+                multiply(UNITS - PACK, HALF, False)
             if UNITS - 1 <= step <= UNITS:
                 quantise(step - 1, 1)
-            for i in range(UNITS // HALF):
-                if step == max(HALF * i + LAG, i + 6):
-                    multiply(HALF * i)
+                multiply(step - 1, 1, step == UNITS)

@@ -117,8 +117,9 @@ def tile_gcn_s_kernel(tc, inputs, adj, W_kernel, W_bias, out):
         xT_banks = {}
         xT_tiles = {}
         feats_banks = {}
-        grouped_feats = {}
-        feats_tiles = {}
+        feats_grouped = const.tile([P, GRAPHS, DIM, PACK], BF16, align_bytes=64)
+        feats_codes = const.tile([P, GRAPHS, DIM], U32, align_bytes=64)
+        feats_scales = const.tile([P, GRAPHS, DIM], U8, align_bytes=64)
 
         def turn_inputs(b):
             xT_ps = bank(BF16)
@@ -141,24 +142,20 @@ def tile_gcn_s_kernel(tc, inputs, adj, W_kernel, W_bias, out):
             feats_banks[b] = feats_ps
 
         def add_bias(b):
-            feats_grouped = graph.tile([P, DIM, PACK], BF16, align_bytes=64, name="feats_grouped")
             nc.vector.tensor_tensor(
-                out=feats_grouped[:],
+                out=feats_grouped[:, b, :, :],
                 in0=feats_banks[b][:].rearrange("p t d -> p d t"),
                 in1=bias_all[:].unsqueeze(2).to_broadcast([P, DIM, PACK]),
                 op=ALU.add,
             )
-            grouped_feats[b] = feats_grouped
 
-        def quantise_feats(b):
-            feats_codes = graph.tile([P, DIM], U32, align_bytes=64, name="feats_codes")
-            feats_scales = graph.tile([P, DIM], U8, align_bytes=64, name="feats_scales")
+        def quantise_feats(first, count):
+            graphs = slice(first, first + count)
             nc.vector.quantize_mx(
-                out=feats_codes[:].bitcast(FP8X4),
-                scales=feats_scales[:],
-                in_=grouped_feats[b][:].rearrange("p d t -> p (d t)"),
+                out=feats_codes[:, graphs, :].rearrange("p b d -> p (b d)").bitcast(FP8X4),
+                scales=feats_scales[:, graphs, :].rearrange("p b d -> p (b d)"),
+                in_=feats_grouped[:, graphs, :, :].rearrange("p b d t -> p (b d t)"),
             )
-            feats_tiles[b] = (feats_codes, feats_scales)
 
         scaled_tiles = {}
         grouped_tiles = []
@@ -183,7 +180,15 @@ def tile_gcn_s_kernel(tc, inputs, adj, W_kernel, W_bias, out):
                 )
             scaled_tiles[unit] = scaled
 
-        def normalise(unit):
+        turned_banks = {}
+
+        def turn(unit):
+            normT_ps = bank(F32)
+            for j in range(PACK):
+                nc.tensor.transpose(normT_ps[:, j, :], scaled_tiles[unit][:, j, :], ident_f32[:])
+            turned_banks[unit] = normT_ps
+
+        def finish(unit):
             b, t = divmod(unit, PACK)
             if t == 0:
                 norm_grouped = graph.tile([P, PACK, P, PACK], BF16, align_bytes=64)
@@ -192,12 +197,9 @@ def tile_gcn_s_kernel(tc, inputs, adj, W_kernel, W_bias, out):
                 codes_tiles.append(norm_codes)
                 norm_scales = graph.tile([P, PACK, P], U8, align_bytes=64)
                 scales_tiles.append(norm_scales)
-            normT_ps = bank(F32)
-            for j in range(PACK):
-                nc.tensor.transpose(normT_ps[:, j, :], scaled_tiles[unit][:, j, :], ident_f32[:])
             nc.vector.tensor_tensor(
                 out=grouped_tiles[b][:, t, :, :],
-                in0=normT_ps[:].rearrange("c j n -> c n j"),
+                in0=turned_banks[unit][:].rearrange("c j n -> c n j"),
                 in1=r_tiles[b][:].unsqueeze(1).to_broadcast([P, P, PACK]),
                 op=ALU.mult,
             )
@@ -213,15 +215,14 @@ def tile_gcn_s_kernel(tc, inputs, adj, W_kernel, W_bias, out):
 
         def multiply(first_unit, count, by_vector):
             b, t0 = divmod(first_unit, PACK)
-            feats_codes, feats_scales = feats_tiles[b]
             out_ps = psum.tile([P, PACK, DIM], F32, name="out_ps", bufs=2)
             for h in range(count):
                 nc.tensor.matmul_mx(
                     out=out_ps[:, h, :],
                     lhsT=codes_tiles[b][:, t0 + h, :].bitcast(FP8X4),
                     lhsT_scale=scales_tiles[b][:, t0 + h, :],
-                    rhs=feats_codes[:].bitcast(FP8X4),
-                    rhs_scale=feats_scales[:],
+                    rhs=feats_codes[:, b, :].bitcast(FP8X4),
+                    rhs_scale=feats_scales[:, b, :],
                     start=True,
                     stop=True,
                 )
@@ -265,27 +266,34 @@ def tile_gcn_s_kernel(tc, inputs, adj, W_kernel, W_bias, out):
         make_feats(2)
         add_bias(1)
         add_bias(2)
-        normalise(0)
+        turn(0)
+        finish(0)
         invert_root(1)
         for unit in range(PACK, BY_GPSIMD):
             scale_rows(unit)
         sum_rows(2)
         take_root(2)
         for unit in range(1, PACK):
-            normalise(unit)
+            turn(unit)
+            finish(unit)
+        turn(PACK)
         for unit in range(BY_GPSIMD, 2 * PACK):
             scale_rows(unit)
-        for b in range(GRAPHS):
-            quantise_feats(b)
+        quantise_feats(0, 2)
+        quantise_feats(2, 1)
         invert_root(2)
         quantise(0, PACK)
         for step in range(PACK, UNITS + 1):
+            if step + 1 < UNITS:
+                turn(step + 1)
             if step < UNITS:
-                normalise(step)
+                finish(step)
             if step + PACK < UNITS:
                 scale_rows(step + PACK)
-            if PACK + HALF <= step < UNITS and step % HALF == 0:
-                quantise(step - HALF, HALF)
+            if step == 2 * PACK:
+                quantise(PACK, PACK)
+            if step == 2 * PACK + HALF:
+                quantise(2 * PACK, HALF)
             if step in (PACK + 3, 2 * PACK + 2):
                 multiply((step // PACK - 1) * PACK, PACK, False)
             if step == UNITS - 1:

@@ -23,9 +23,8 @@ FLOPS = 2 * GRAPHS * NODES * (NODES * DIM + FEATS * DIM)
 
 UNITS = GRAPHS * PACK
 HALF = 2
-BY_GPSIMD = 6
-WARM_UP = 14
-BLOCK = 8
+WARM_UP = 48
+SCALAR_UNITS = (0, 2)
 
 
 def tile_gcn_s_kernel(tc, inputs, adj, W_kernel, W_bias, out):
@@ -45,72 +44,81 @@ def tile_gcn_s_kernel(tc, inputs, adj, W_kernel, W_bias, out):
         for b in range(GRAPHS):
             adj_sb = graph.tile([P, PACK, NODES], BF16)
             adj_tiles.append(adj_sb)
+
+        def load_adj(b, size):
             adj_rows = adj[b].rearrange("(p t) m -> p t m", t=PACK)
-            size = 1 if b == 0 else HALF
             for t in range(0, PACK, size):
-                nc.sync.dma_start(out=adj_sb[:, t : t + size, :], in_=adj_rows[:, t : t + size, :])
-            if b == 0:
-                nc.sync.dma_start(out=w_sb[:], in_=W_kernel)
                 nc.sync.dma_start(
-                    out=bias_row[0:1, :], in_=W_bias.rearrange("(o d) -> o d", o=1)
+                    out=adj_tiles[b][:, t : t + size, :], in_=adj_rows[:, t : t + size, :]
                 )
-                for g in range(GRAPHS):
-                    nc.sync.dma_start(
-                        out=x_sb[:, g, :, :], in_=inputs[g].rearrange("(p t) f -> p t f", t=PACK)
-                    )
+
+        load_adj(0, 1)
+        load_adj(1, HALF)
+        load_adj(2, HALF)
+        nc.sync.dma_start(out=bias_row[0:1, :], in_=W_bias.rearrange("(o d) -> o d", o=1))
+        nc.sync.dma_start(out=w_sb[:], in_=W_kernel)
+        for g in range(GRAPHS):
+            nc.sync.dma_start(
+                out=x_sb[:, g, :, :], in_=inputs[g].rearrange("(p t) f -> p t f", t=PACK)
+            )
 
         one = const.tile([P, 1], F32)
         nc.vector.memset(one[:], 1.0)
         warm = const.tile([P, 1], F32)
         nc.scalar.activation(out=warm[:], in_=one[:], func=FUNC.Sqrt)
-        ones = const.tile([P, P], BF16)
+        ones = const.tile([P, 1], BF16)
         nc.gpsimd.memset(ones[:], 1.0)
         ident_bf = const.tile([P, P], BF16)
         make_identity(nc, ident_bf[:])
         ident_f32 = const.tile([P, P], F32)
         make_identity(nc, ident_f32[:])
 
-        def bank(dtype):
-            return psum.tile([P, PACK, P], dtype, name="bank", tag="bank", bufs=6)
+        def turn_bank(dtype):
+            return psum.tile([P, PACK, P], dtype, name="turn_bank", tag="turn_bank", bufs=3)
 
-        degree_views = []
-        r_tiles = []
+        def feats_bank(dtype):
+            return psum.tile([P, PACK, P], dtype, name="feats_bank", tag="feats_bank", bufs=3)
 
-        def sum_rows(b):
-            degree = graph.tile([P, 2, BLOCK], F32)
-            degree_views.append(degree[:, :, 0 : PACK // 2].rearrange("p e i -> p i e"))
-            for t in range(PACK):
-                rows = adj_tiles[b][:, t, :]
-                total = degree[:, t % 2, t // 2 : t // 2 + 1]
-                if b == 0 and t % 2 == 1:
-                    nc.vector.reduce_sum(out=total, in_=rows, axis=mybir.AxisListType.X)
-                else:
-                    unused = work.tile([P, NODES], BF16)
-                    nc.scalar.activation(
-                        out=unused[:], in_=rows, func=FUNC.Copy, accum_out=total
-                    )
-
+        degree_tiles = []
         root_tiles = []
-        pairs = "p (i e) -> p i e"
+        r_tiles = []
+        for b in range(GRAPHS):
+            degree = graph.tile([P, PACK], F32, name="degree")
+            degree_tiles.append(degree)
+
+        def degree_at(b, t):
+            return degree_tiles[b][:, t : t + 1]
+
+        def sum_by_scalar(b, t):
+            unused = work.tile([P, NODES], BF16, name="unused_s")
+            nc.scalar.activation(
+                out=unused[:], in_=adj_tiles[b][:, t, :], func=FUNC.Copy, accum_out=degree_at(b, t)
+            )
+
+        def sum_by_vector(b, t):
+            unused = work.tile([P, NODES], BF16, name="unused_v")
+            nc.vector.tensor_scalar(
+                out=unused[:], in0=adj_tiles[b][:, t, :], scalar1=1.0, scalar2=None,
+                op0=ALU.mult, op1=ALU.add, accum_out=degree_at(b, t),
+            )
 
         def take_root(b):
             root = graph.tile([P, PACK], F32, name="root")
-            nc.scalar.activation(
-                out=root[:].rearrange(pairs, e=2), in_=degree_views[b], func=FUNC.Sqrt
-            )
+            nc.scalar.activation(out=root[:], in_=degree_tiles[b][:], func=FUNC.Sqrt)
             root_tiles.append(root)
 
-        def invert_root(b):
-            positive = graph.tile([P, PACK], F32, name="positive")
-            nc.vector.tensor_single_scalar(
-                out=positive[:].rearrange(pairs, e=2), in_=degree_views[b], scalar=0.0,
-                op=ALU.is_gt,
-            )
+        inverse_tiles = []
+
+        def invert(b):
             inverse = graph.tile([P, PACK], F32, name="inverse")
-            nc.vector.reciprocal(out=inverse[:], in_=root_tiles[b][:])
+            nc.vector.reciprocal(out=inverse[:], in_=degree_tiles[b][:])
+            inverse_tiles.append(inverse)
+
+        def make_r(b):
             r = graph.tile([P, PACK], F32, name="r")
             nc.vector.scalar_tensor_tensor(
-                out=r[:], in0=inverse[:], scalar=HUGE, in1=positive[:], op0=ALU.min, op1=ALU.mult
+                out=r[:], in0=inverse_tiles[b][:], scalar=HUGE, in1=root_tiles[b][:],
+                op0=ALU.min, op1=ALU.mult,
             )
             r_tiles.append(r)
 
@@ -122,31 +130,32 @@ def tile_gcn_s_kernel(tc, inputs, adj, W_kernel, W_bias, out):
         feats_scales = const.tile([P, GRAPHS, DIM], U8, align_bytes=64)
 
         def turn_inputs(b):
-            xT_ps = bank(BF16)
+            xT_ps = feats_bank(BF16)
             for t in range(PACK):
                 nc.tensor.transpose(xT_ps[:, t, :], x_sb[:, b, t, :], ident_bf[:])
             xT_banks[b] = xT_ps
 
         def copy_inputs(b):
             xT_sb = graph.tile([FEATS, PACK, P], BF16, name="xT_sb")
-            nc.vector.tensor_copy(out=xT_sb[:], in_=xT_banks[b][:])
+            nc.scalar.copy(out=xT_sb[:], in_=xT_banks[b][:])
             xT_tiles[b] = xT_sb
 
         def make_feats(b):
-            feats_ps = bank(F32)
+            feats_ps = feats_bank(F32)
             for t in range(PACK):
                 nc.tensor.matmul(
+                    out=feats_ps[:, t, :], lhsT=bias_col[:].to_broadcast([P, P]), rhs=ident_f32[:],
+                    is_transpose=True, start=True, stop=False,
+                )
+                nc.tensor.matmul(
                     out=feats_ps[:, t, :], lhsT=xT_tiles[b][:, t, :], rhs=w_sb[:],
-                    start=True, stop=True,
+                    start=False, stop=True,
                 )
             feats_banks[b] = feats_ps
 
-        def add_bias(b):
-            nc.vector.tensor_tensor(
-                out=feats_grouped[:, b, :, :],
-                in0=feats_banks[b][:].rearrange("p t d -> p d t"),
-                in1=bias_all[:].unsqueeze(2).to_broadcast([P, DIM, PACK]),
-                op=ALU.add,
+        def round_feats(b):
+            nc.scalar.copy(
+                out=feats_grouped[:, b, :, :], in_=feats_banks[b][:].rearrange("p t d -> p d t")
             )
 
         def quantise_feats(first, count):
@@ -162,18 +171,15 @@ def tile_gcn_s_kernel(tc, inputs, adj, W_kernel, W_bias, out):
         codes_tiles = []
         scales_tiles = []
 
-        def by_scalar(unit):
-            return unit >= BY_GPSIMD
-
         def scale_rows(unit):
             b, t = divmod(unit, PACK)
             columns = adj_tiles[b][:, t, :].rearrange("p (c j) -> p j c", j=PACK)
             factor = r_tiles[b][:, t : t + 1]
-            if by_scalar(unit):
+            if unit in SCALAR_UNITS:
                 scaled = work.tile([P, PACK, P], F32, name="scaled_s", bufs=4)
                 nc.scalar.activation(out=scaled[:], in_=columns, func=FUNC.Copy, scale=factor)
             else:
-                scaled = work.tile([P, PACK, P], F32, name="scaled_g", bufs=BY_GPSIMD)
+                scaled = work.tile([P, PACK, P], F32, name="scaled_g", bufs=10)
                 nc.gpsimd.tensor_scalar(
                     out=scaled[:], in0=columns, scalar1=factor, scalar2=0.0,
                     op0=ALU.mult, op1=ALU.add,
@@ -183,7 +189,7 @@ def tile_gcn_s_kernel(tc, inputs, adj, W_kernel, W_bias, out):
         turned_banks = {}
 
         def turn(unit):
-            normT_ps = bank(F32)
+            normT_ps = turn_bank(F32)
             for j in range(PACK):
                 nc.tensor.transpose(normT_ps[:, j, :], scaled_tiles[unit][:, j, :], ident_f32[:])
             turned_banks[unit] = normT_ps
@@ -238,66 +244,87 @@ def tile_gcn_s_kernel(tc, inputs, adj, W_kernel, W_bias, out):
             out_rows = out[b].rearrange("(p t) d -> p t d", t=PACK)
             nc.sync.dma_start(out=out_rows[:, t0 : t0 + count, :], in_=out_sb[:, 0:count, :])
 
-        idle_ps = bank(BF16)
+        idle_ps = feats_bank(BF16)
         for i in range(WARM_UP):
             nc.tensor.transpose(idle_ps[:, i % PACK, :], ident_bf[:], ident_bf[:])
-        sum_rows(0)
-        bias_ps = bank(F32)
-        nc.tensor.matmul(
-            out=bias_ps[:, 0, :], lhsT=ones[:], rhs=bias_row[:], start=True, stop=True
-        )
-        bias_all = const.tile([P, DIM], F32)
-        nc.scalar.copy(out=bias_all[:], in_=bias_ps[:, 0, :])
-        turn_inputs(0)
-        copy_inputs(0)
+        sum_by_vector(0, 0)
+        sum_by_scalar(0, 1)
+        sum_by_vector(0, 2)
+        sum_by_vector(0, 3)
         take_root(0)
-        invert_root(0)
-        for unit in range(PACK):
-            scale_rows(unit)
-        turn_inputs(1)
-        make_feats(0)
-        copy_inputs(1)
-        turn_inputs(2)
-        make_feats(1)
-        sum_rows(1)
-        take_root(1)
-        add_bias(0)
-        copy_inputs(2)
-        make_feats(2)
-        add_bias(1)
-        add_bias(2)
+        invert(0)
+        make_r(0)
+        scale_rows(0)
+        scale_rows(1)
+        scale_rows(3)
+        sum_by_vector(1, 0)
+        sum_by_scalar(1, 1)
+        sum_by_vector(1, 2)
+        sum_by_vector(1, 3)
         turn(0)
         finish(0)
-        invert_root(1)
-        for unit in range(PACK, BY_GPSIMD):
+        take_root(1)
+        invert(1)
+        scale_rows(2)
+        turn(1)
+        finish(1)
+        make_r(1)
+        for unit in range(PACK, 2 * PACK):
             scale_rows(unit)
-        sum_rows(2)
+        for t in range(PACK):
+            sum_by_scalar(2, t)
         take_root(2)
-        for unit in range(1, PACK):
-            turn(unit)
-            finish(unit)
-        turn(PACK)
-        for unit in range(BY_GPSIMD, 2 * PACK):
-            scale_rows(unit)
-        quantise_feats(0, 2)
-        quantise_feats(2, 1)
-        invert_root(2)
+        turn(2)
+        finish(2)
+        bias_ps = feats_bank(F32)
+        nc.tensor.matmul(
+            out=bias_ps[:, 0, 0:1], lhsT=bias_row[:], rhs=ones[:], start=True, stop=True
+        )
+        bias_col = const.tile([P, 1], F32)
+        nc.scalar.copy(out=bias_col[:], in_=bias_ps[:, 0, 0:1])
+        turn(3)
+        finish(3)
+        turn_inputs(0)
+        copy_inputs(0)
+        turn_inputs(1)
+        copy_inputs(1)
+        turn(4)
+        finish(4)
+        invert(2)
+        turn(5)
         quantise(0, PACK)
-        for step in range(PACK, UNITS + 1):
-            if step + 1 < UNITS:
-                turn(step + 1)
-            if step < UNITS:
-                finish(step)
-            if step + PACK < UNITS:
-                scale_rows(step + PACK)
-            if step == 2 * PACK:
-                quantise(PACK, PACK)
-            if step == 2 * PACK + HALF:
-                quantise(2 * PACK, HALF)
-            if step in (PACK + 3, 2 * PACK + 2):
-                multiply((step // PACK - 1) * PACK, PACK, False)
-            if step == UNITS - 1:
-                multiply(UNITS - PACK, HALF, False)
-            if UNITS - 1 <= step <= UNITS:
-                quantise(step - 1, 1)
-                multiply(step - 1, 1, step == UNITS)
+        make_r(2)
+        for unit in range(2 * PACK, UNITS):
+            scale_rows(unit)
+        finish(5)
+        turn(6)
+        turn_inputs(2)
+        copy_inputs(2)
+        finish(6)
+        make_feats(0)
+        round_feats(0)
+        turn(7)
+        finish(7)
+        make_feats(1)
+        round_feats(1)
+        turn(8)
+        finish(8)
+        quantise(PACK, PACK)
+        turn(9)
+        finish(9)
+        make_feats(2)
+        round_feats(2)
+        quantise_feats(0, 2)
+        turn(10)
+        finish(10)
+        turn(11)
+        multiply(0, PACK, False)
+        quantise_feats(2, 1)
+        quantise(2 * PACK, HALF)
+        finish(11)
+        multiply(PACK, PACK, False)
+        multiply(2 * PACK, HALF, False)
+        quantise(10, 1)
+        multiply(10, 1, False)
+        quantise(11, 1)
+        multiply(11, 1, True)

@@ -17,14 +17,13 @@ FEATS = 128
 DIM = 128
 P = 128
 PACK = 4
+PAIR = 2
 HUGE = 3.0e38
 
 FLOPS = 2 * GRAPHS * NODES * (NODES * DIM + FEATS * DIM)
 
 UNITS = GRAPHS * PACK
 HALF = 2
-WARM_UP = 48
-SCALAR_UNITS = (0, 2)
 
 
 def tile_gcn_s_kernel(tc, inputs, adj, W_kernel, W_bias, out):
@@ -38,7 +37,7 @@ def tile_gcn_s_kernel(tc, inputs, adj, W_kernel, W_bias, out):
 
         w_sb = const.tile([FEATS, DIM], BF16)
         bias_row = const.tile([P, DIM], BF16)
-        x_sb = const.tile([P, GRAPHS, PACK, FEATS], BF16)
+        x_sb = const.tile([P, GRAPHS, HALF, PAIR, FEATS], BF16)
         nc.gpsimd.memset(bias_row[:], 0.0)
         adj_tiles = []
         for b in range(GRAPHS):
@@ -52,62 +51,60 @@ def tile_gcn_s_kernel(tc, inputs, adj, W_kernel, W_bias, out):
                     out=adj_tiles[b][:, t : t + size, :], in_=adj_rows[:, t : t + size, :]
                 )
 
+        def load_inputs(b):
+            nc.sync.dma_start(
+                out=x_sb[:, b, :, :, :],
+                in_=inputs[b].rearrange("(u c e) f -> c u e f", u=HALF, e=PAIR),
+            )
+
         load_adj(0, 1)
+        nc.sync.dma_start(out=bias_row[0:1, :], in_=W_bias.rearrange("(o d) -> o d", o=1))
+        for b in range(GRAPHS):
+            load_inputs(b)
+        nc.sync.dma_start(out=w_sb[:], in_=W_kernel)
         load_adj(1, HALF)
         load_adj(2, HALF)
-        nc.sync.dma_start(out=bias_row[0:1, :], in_=W_bias.rearrange("(o d) -> o d", o=1))
-        nc.sync.dma_start(out=w_sb[:], in_=W_kernel)
-        for g in range(GRAPHS):
-            nc.sync.dma_start(
-                out=x_sb[:, g, :, :], in_=inputs[g].rearrange("(p t) f -> p t f", t=PACK)
-            )
 
         one = const.tile([P, 1], F32)
         nc.vector.memset(one[:], 1.0)
         warm = const.tile([P, 1], F32)
         nc.scalar.activation(out=warm[:], in_=one[:], func=FUNC.Sqrt)
-        ones = const.tile([P, 1], BF16)
+        ones = const.tile([P, P], BF16)
         nc.gpsimd.memset(ones[:], 1.0)
         ident_bf = const.tile([P, P], BF16)
         make_identity(nc, ident_bf[:])
         ident_f32 = const.tile([P, P], F32)
         make_identity(nc, ident_f32[:])
 
-        def turn_bank(dtype):
-            return psum.tile([P, PACK, P], dtype, name="turn_bank", tag="turn_bank", bufs=3)
-
         def feats_bank(dtype):
-            return psum.tile([P, PACK, P], dtype, name="feats_bank", tag="feats_bank", bufs=3)
+            return psum.tile([P, PACK, P], dtype, name="feats_bank", tag="feats_bank", bufs=2)
 
         degree_tiles = []
         root_tiles = []
+        inverse_tiles = []
         r_tiles = []
         for b in range(GRAPHS):
             degree = graph.tile([P, PACK], F32, name="degree")
             degree_tiles.append(degree)
 
-        def degree_at(b, t):
-            return degree_tiles[b][:, t : t + 1]
-
         def sum_by_scalar(b, t):
             unused = work.tile([P, NODES], BF16, name="unused_s")
             nc.scalar.activation(
-                out=unused[:], in_=adj_tiles[b][:, t, :], func=FUNC.Copy, accum_out=degree_at(b, t)
+                out=unused[:], in_=adj_tiles[b][:, t, :], func=FUNC.Copy,
+                accum_out=degree_tiles[b][:, t : t + 1],
             )
 
         def sum_by_vector(b, t):
             unused = work.tile([P, NODES], BF16, name="unused_v")
             nc.vector.tensor_scalar(
                 out=unused[:], in0=adj_tiles[b][:, t, :], scalar1=1.0, scalar2=None,
-                op0=ALU.mult, op1=ALU.add, accum_out=degree_at(b, t),
+                op0=ALU.mult, op1=ALU.add, accum_out=degree_tiles[b][:, t : t + 1],
             )
 
         def take_root(b):
             root = graph.tile([P, PACK], F32, name="root")
             nc.scalar.activation(out=root[:], in_=degree_tiles[b][:], func=FUNC.Sqrt)
             root_tiles.append(root)
-
-        inverse_tiles = []
 
         def invert(b):
             inverse = graph.tile([P, PACK], F32, name="inverse")
@@ -122,6 +119,16 @@ def tile_gcn_s_kernel(tc, inputs, adj, W_kernel, W_bias, out):
             )
             r_tiles.append(r)
 
+        spread_banks = []
+
+        def spread(b):
+            r_ps = psum.tile([P, PACK, P], F32, name="r_ps", bufs=2)
+            for t in range(PACK):
+                nc.tensor.transpose(
+                    r_ps[:, t, :], r_tiles[b][:, t : t + 1].to_broadcast([P, P]), ident_f32[:]
+                )
+            spread_banks.append(r_ps)
+
         xT_banks = {}
         xT_tiles = {}
         feats_banks = {}
@@ -131,8 +138,9 @@ def tile_gcn_s_kernel(tc, inputs, adj, W_kernel, W_bias, out):
 
         def turn_inputs(b):
             xT_ps = feats_bank(BF16)
-            for t in range(PACK):
-                nc.tensor.transpose(xT_ps[:, t, :], x_sb[:, b, t, :], ident_bf[:])
+            for j in range(PACK):
+                u, e = divmod(j, PAIR)
+                nc.tensor.transpose(xT_ps[:, j, :], x_sb[:, b, u, e, :], ident_bf[:])
             xT_banks[b] = xT_ps
 
         def copy_inputs(b):
@@ -142,72 +150,73 @@ def tile_gcn_s_kernel(tc, inputs, adj, W_kernel, W_bias, out):
 
         def make_feats(b):
             feats_ps = feats_bank(F32)
-            for t in range(PACK):
+            for j in range(PACK):
                 nc.tensor.matmul(
-                    out=feats_ps[:, t, :], lhsT=bias_col[:].to_broadcast([P, P]), rhs=ident_f32[:],
-                    is_transpose=True, start=True, stop=False,
-                )
-                nc.tensor.matmul(
-                    out=feats_ps[:, t, :], lhsT=xT_tiles[b][:, t, :], rhs=w_sb[:],
-                    start=False, stop=True,
+                    out=feats_ps[:, j, :], lhsT=xT_tiles[b][:, j, :], rhs=w_sb[:],
+                    start=True, stop=True,
                 )
             feats_banks[b] = feats_ps
 
-        def round_feats(b):
-            nc.scalar.copy(
-                out=feats_grouped[:, b, :, :], in_=feats_banks[b][:].rearrange("p t d -> p d t")
+        def add_bias(b):
+            nc.vector.tensor_tensor(
+                out=feats_grouped[:, b, :, :],
+                in0=feats_banks[b][:].rearrange("c j d -> c d j"),
+                in1=bias_all[:].unsqueeze(2).to_broadcast([P, DIM, PACK]),
+                op=ALU.add,
             )
 
         def quantise_feats(first, count):
             graphs = slice(first, first + count)
             nc.vector.quantize_mx(
-                out=feats_codes[:, graphs, :].rearrange("p b d -> p (b d)").bitcast(FP8X4),
-                scales=feats_scales[:, graphs, :].rearrange("p b d -> p (b d)"),
-                in_=feats_grouped[:, graphs, :, :].rearrange("p b d t -> p (b d t)"),
+                out=feats_codes[:, graphs, :].rearrange("c b d -> c (b d)").bitcast(FP8X4),
+                scales=feats_scales[:, graphs, :].rearrange("c b d -> c (b d)"),
+                in_=feats_grouped[:, graphs, :, :].rearrange("c b d j -> c (b d j)"),
             )
 
-        scaled_tiles = {}
+        norm_tiles = {}
+        word_banks = {}
         grouped_tiles = []
         codes_tiles = []
         scales_tiles = []
 
-        def scale_rows(unit):
+        def normalise(unit):
             b, t = divmod(unit, PACK)
-            columns = adj_tiles[b][:, t, :].rearrange("p (c j) -> p j c", j=PACK)
-            factor = r_tiles[b][:, t : t + 1]
-            if unit in SCALAR_UNITS:
-                scaled = work.tile([P, PACK, P], F32, name="scaled_s", bufs=4)
-                nc.scalar.activation(out=scaled[:], in_=columns, func=FUNC.Copy, scale=factor)
-            else:
-                scaled = work.tile([P, PACK, P], F32, name="scaled_g", bufs=10)
-                nc.gpsimd.tensor_scalar(
-                    out=scaled[:], in0=columns, scalar1=factor, scalar2=0.0,
-                    op0=ALU.mult, op1=ALU.add,
-                )
-            scaled_tiles[unit] = scaled
+            norm = work.tile([P, NODES], BF16, name="norm", bufs=4)
+            split = "p (q t) -> p q t"
+            nc.vector.scalar_tensor_tensor(
+                out=norm[:].rearrange(split, t=PACK),
+                in0=adj_tiles[b][:, t, :].rearrange(split, t=PACK),
+                scalar=r_tiles[b][:, t : t + 1],
+                in1=spread_banks[b][:].rearrange("p t q -> p q t"),
+                op0=ALU.mult, op1=ALU.mult,
+            )
+            norm_tiles[unit] = norm
 
-        turned_banks = {}
+        def turn(first_unit, count):
+            word_ps = psum.tile([P, HALF, HALF, P], F32, name="word_ps", bufs=2)
+            for h in range(count):
+                words = norm_tiles[first_unit + h][:].bitcast(F32)
+                for u in range(HALF):
+                    nc.tensor.transpose(
+                        word_ps[:, h, u, :], words[:, u * P : (u + 1) * P], ident_f32[:]
+                    )
+            word_banks[first_unit] = word_ps
 
-        def turn(unit):
-            normT_ps = turn_bank(F32)
-            for j in range(PACK):
-                nc.tensor.transpose(normT_ps[:, j, :], scaled_tiles[unit][:, j, :], ident_f32[:])
-            turned_banks[unit] = normT_ps
-
-        def finish(unit):
-            b, t = divmod(unit, PACK)
-            if t == 0:
+        def group(first_unit, count, by_vector=False):
+            b, t0 = divmod(first_unit, PACK)
+            if t0 == 0:
                 norm_grouped = graph.tile([P, PACK, P, PACK], BF16, align_bytes=64)
                 grouped_tiles.append(norm_grouped)
                 norm_codes = graph.tile([P, PACK, P], U32, align_bytes=64)
                 codes_tiles.append(norm_codes)
                 norm_scales = graph.tile([P, PACK, P], U8, align_bytes=64)
                 scales_tiles.append(norm_scales)
-            nc.vector.tensor_tensor(
-                out=grouped_tiles[b][:, t, :, :],
-                in0=turned_banks[unit][:].rearrange("c j n -> c n j"),
-                in1=r_tiles[b][:].unsqueeze(1).to_broadcast([P, P, PACK]),
-                op=ALU.mult,
+            copy = nc.vector.tensor_copy if by_vector else nc.scalar.copy
+            copy(
+                out=grouped_tiles[b][:, t0 : t0 + count, :, :]
+                .rearrange("c t n j -> c (t n j)").bitcast(F32)
+                .rearrange("c (t n u) -> c t n u", n=P, u=HALF),
+                in_=word_banks[first_unit][:, 0:count, :, :].rearrange("c t u n -> c t n u"),
             )
 
         def quantise(first_unit, count):
@@ -244,9 +253,6 @@ def tile_gcn_s_kernel(tc, inputs, adj, W_kernel, W_bias, out):
             out_rows = out[b].rearrange("(p t) d -> p t d", t=PACK)
             nc.sync.dma_start(out=out_rows[:, t0 : t0 + count, :], in_=out_sb[:, 0:count, :])
 
-        idle_ps = feats_bank(BF16)
-        for i in range(WARM_UP):
-            nc.tensor.transpose(idle_ps[:, i % PACK, :], ident_bf[:], ident_bf[:])
         sum_by_vector(0, 0)
         sum_by_scalar(0, 1)
         sum_by_vector(0, 2)
@@ -254,77 +260,75 @@ def tile_gcn_s_kernel(tc, inputs, adj, W_kernel, W_bias, out):
         take_root(0)
         invert(0)
         make_r(0)
-        scale_rows(0)
-        scale_rows(1)
-        scale_rows(3)
+        bias_ps = feats_bank(F32)
+        nc.tensor.matmul(
+            out=bias_ps[:, 0, :], lhsT=ones[:], rhs=bias_row[:], start=True, stop=True
+        )
+        bias_all = const.tile([P, DIM], F32)
+        nc.scalar.copy(out=bias_all[:], in_=bias_ps[:, 0, :])
+        turn_inputs(0)
+        copy_inputs(0)
+        spread(0)
+        turn_inputs(1)
         sum_by_vector(1, 0)
         sum_by_scalar(1, 1)
         sum_by_vector(1, 2)
-        sum_by_vector(1, 3)
-        turn(0)
-        finish(0)
-        take_root(1)
-        invert(1)
-        scale_rows(2)
-        turn(1)
-        finish(1)
-        make_r(1)
-        for unit in range(PACK, 2 * PACK):
-            scale_rows(unit)
-        for t in range(PACK):
-            sum_by_scalar(2, t)
-        take_root(2)
-        turn(2)
-        finish(2)
-        bias_ps = feats_bank(F32)
-        nc.tensor.matmul(
-            out=bias_ps[:, 0, 0:1], lhsT=bias_row[:], rhs=ones[:], start=True, stop=True
-        )
-        bias_col = const.tile([P, 1], F32)
-        nc.scalar.copy(out=bias_col[:], in_=bias_ps[:, 0, 0:1])
-        turn(3)
-        finish(3)
-        turn_inputs(0)
-        copy_inputs(0)
-        turn_inputs(1)
+        sum_by_scalar(1, 3)
         copy_inputs(1)
-        turn(4)
-        finish(4)
-        invert(2)
-        turn(5)
-        quantise(0, PACK)
-        make_r(2)
-        for unit in range(2 * PACK, UNITS):
-            scale_rows(unit)
-        finish(5)
-        turn(6)
+        take_root(1)
         turn_inputs(2)
         copy_inputs(2)
-        finish(6)
         make_feats(0)
-        round_feats(0)
-        turn(7)
-        finish(7)
+        normalise(0)
+        invert(1)
+        normalise(1)
+        turn(0, HALF)
+        make_r(1)
+        spread(1)
+        sum_by_scalar(2, 0)
+        normalise(2)
+        group(0, HALF)
+        add_bias(0)
         make_feats(1)
-        round_feats(1)
-        turn(8)
-        finish(8)
-        quantise(PACK, PACK)
-        turn(9)
-        finish(9)
+        normalise(3)
+        turn(2, HALF)
+        sum_by_scalar(2, 1)
+        sum_by_scalar(2, 2)
+        normalise(4)
+        group(2, HALF)
+        sum_by_scalar(2, 3)
+        take_root(2)
+        normalise(5)
+        turn(4, HALF)
+        add_bias(1)
         make_feats(2)
-        round_feats(2)
+        normalise(6)
+        group(4, HALF)
+        invert(2)
+        normalise(7)
+        make_r(2)
+        turn(6, HALF)
+        spread(2)
+        quantise(0, PACK)
+        group(6, HALF)
         quantise_feats(0, 2)
-        turn(10)
-        finish(10)
-        turn(11)
+        add_bias(2)
+        normalise(8)
         multiply(0, PACK, False)
-        quantise_feats(2, 1)
-        quantise(2 * PACK, HALF)
-        finish(11)
+        normalise(9)
+        turn(8, HALF)
+        quantise(PACK, PACK)
+        group(8, HALF)
+        normalise(10)
         multiply(PACK, PACK, False)
-        multiply(2 * PACK, HALF, False)
-        quantise(10, 1)
+        turn(10, 1)
+        normalise(11)
+        group(10, 1)
+        turn(11, 1)
+        quantise_feats(2, 1)
+        quantise(8, HALF)
+        group(11, 1, True)
+        multiply(8, HALF, False)
+        quantise(10, HALF)
         multiply(10, 1, False)
-        quantise(11, 1)
         multiply(11, 1, True)

@@ -58,26 +58,26 @@ def tile_gcn_s_kernel(tc, inputs, adj, W_kernel, W_bias, out):
             )
 
         load_adj(0, 1)
+        load_adj(1, HALF)
         nc.sync.dma_start(out=bias_row[0:1, :], in_=W_bias.rearrange("(o d) -> o d", o=1))
         for b in range(GRAPHS):
             load_inputs(b)
         nc.sync.dma_start(out=w_sb[:], in_=W_kernel)
-        load_adj(1, HALF)
         load_adj(2, HALF)
 
         one = const.tile([P, 1], F32)
         nc.vector.memset(one[:], 1.0)
         warm = const.tile([P, 1], F32)
         nc.scalar.activation(out=warm[:], in_=one[:], func=FUNC.Sqrt)
-        ones = const.tile([P, P], BF16)
+        ones = const.tile([P, 1], BF16)
         nc.gpsimd.memset(ones[:], 1.0)
         ident_bf = const.tile([P, P], BF16)
         make_identity(nc, ident_bf[:])
         ident_f32 = const.tile([P, P], F32)
         make_identity(nc, ident_f32[:])
 
-        def feats_bank(dtype):
-            return psum.tile([P, PACK, P], dtype, name="feats_bank", tag="feats_bank", bufs=2)
+        def bank(dtype):
+            return psum.tile([P, PACK, P], dtype, name="bank", tag="bank", bufs=4)
 
         degree_tiles = []
         root_tiles = []
@@ -99,6 +99,24 @@ def tile_gcn_s_kernel(tc, inputs, adj, W_kernel, W_bias, out):
             nc.vector.tensor_scalar(
                 out=unused[:], in0=adj_tiles[b][:, t, :], scalar1=1.0, scalar2=None,
                 op0=ALU.mult, op1=ALU.add, accum_out=degree_tiles[b][:, t : t + 1],
+            )
+
+        half_sums = {}
+
+        def add_halves(b, t):
+            rows = adj_tiles[b][:, t, :]
+            half_sum = work.tile([P, NODES // 2], F32, name="half_sum", bufs=4)
+            nc.gpsimd.tensor_tensor(
+                out=half_sum[:], in0=rows[:, 0 : NODES // 2], in1=rows[:, NODES // 2 : NODES],
+                op=ALU.add,
+            )
+            half_sums[b, t] = half_sum
+
+        def sum_halves(b, t):
+            unused = work.tile([P, NODES // 2], F32, name="unused_h")
+            nc.scalar.activation(
+                out=unused[:], in_=half_sums[b, t][:], func=FUNC.Copy,
+                accum_out=degree_tiles[b][:, t : t + 1],
             )
 
         def take_root(b):
@@ -137,7 +155,7 @@ def tile_gcn_s_kernel(tc, inputs, adj, W_kernel, W_bias, out):
         feats_scales = const.tile([P, GRAPHS, DIM], U8, align_bytes=64)
 
         def turn_inputs(b):
-            xT_ps = feats_bank(BF16)
+            xT_ps = bank(BF16)
             for j in range(PACK):
                 u, e = divmod(j, PAIR)
                 nc.tensor.transpose(xT_ps[:, j, :], x_sb[:, b, u, e, :], ident_bf[:])
@@ -149,20 +167,21 @@ def tile_gcn_s_kernel(tc, inputs, adj, W_kernel, W_bias, out):
             xT_tiles[b] = xT_sb
 
         def make_feats(b):
-            feats_ps = feats_bank(F32)
+            feats_ps = bank(F32)
             for j in range(PACK):
                 nc.tensor.matmul(
+                    out=feats_ps[:, j, :], lhsT=bias_col[:].to_broadcast([P, P]), rhs=ident_f32[:],
+                    is_transpose=True, start=True, stop=False,
+                )
+                nc.tensor.matmul(
                     out=feats_ps[:, j, :], lhsT=xT_tiles[b][:, j, :], rhs=w_sb[:],
-                    start=True, stop=True,
+                    start=False, stop=True,
                 )
             feats_banks[b] = feats_ps
 
-        def add_bias(b):
-            nc.vector.tensor_tensor(
-                out=feats_grouped[:, b, :, :],
-                in0=feats_banks[b][:].rearrange("c j d -> c d j"),
-                in1=bias_all[:].unsqueeze(2).to_broadcast([P, DIM, PACK]),
-                op=ALU.add,
+        def round_feats(b):
+            nc.scalar.copy(
+                out=feats_grouped[:, b, :, :], in_=feats_banks[b][:].rearrange("c j d -> c d j")
             )
 
         def quantise_feats(first, count):
@@ -230,7 +249,7 @@ def tile_gcn_s_kernel(tc, inputs, adj, W_kernel, W_bias, out):
 
         def multiply(first_unit, count, by_vector):
             b, t0 = divmod(first_unit, PACK)
-            out_ps = psum.tile([P, PACK, DIM], F32, name="out_ps", bufs=2)
+            out_ps = bank(F32)
             for h in range(count):
                 nc.tensor.matmul_mx(
                     out=out_ps[:, h, :],
@@ -260,69 +279,70 @@ def tile_gcn_s_kernel(tc, inputs, adj, W_kernel, W_bias, out):
         take_root(0)
         invert(0)
         make_r(0)
-        bias_ps = feats_bank(F32)
-        nc.tensor.matmul(
-            out=bias_ps[:, 0, :], lhsT=ones[:], rhs=bias_row[:], start=True, stop=True
-        )
-        bias_all = const.tile([P, DIM], F32)
-        nc.scalar.copy(out=bias_all[:], in_=bias_ps[:, 0, :])
-        turn_inputs(0)
-        copy_inputs(0)
         spread(0)
-        turn_inputs(1)
-        sum_by_vector(1, 0)
-        sum_by_scalar(1, 1)
-        sum_by_vector(1, 2)
-        sum_by_scalar(1, 3)
-        copy_inputs(1)
+        sum_by_scalar(1, 0)
+        sum_by_vector(1, 1)
+        sum_by_scalar(1, 2)
+        sum_by_vector(1, 3)
+        bias_ps = bank(F32)
+        nc.tensor.matmul(
+            out=bias_ps[:, 0, 0:1], lhsT=bias_row[:], rhs=ones[:], start=True, stop=True
+        )
+        bias_col = const.tile([P, 1], F32)
+        nc.scalar.copy(out=bias_col[:], in_=bias_ps[:, 0, 0:1])
         take_root(1)
-        turn_inputs(2)
-        copy_inputs(2)
-        make_feats(0)
+        turn_inputs(0)
+        turn_inputs(1)
+        for t in range(PACK):
+            add_halves(2, t)
         normalise(0)
+        copy_inputs(0)
         invert(1)
         normalise(1)
-        turn(0, HALF)
+        copy_inputs(1)
         make_r(1)
+        turn(0, HALF)
         spread(1)
-        sum_by_scalar(2, 0)
+        make_feats(0)
         normalise(2)
+        sum_halves(2, 0)
         group(0, HALF)
-        add_bias(0)
-        make_feats(1)
         normalise(3)
         turn(2, HALF)
-        sum_by_scalar(2, 1)
-        sum_by_scalar(2, 2)
-        normalise(4)
-        group(2, HALF)
-        sum_by_scalar(2, 3)
+        for t in range(1, PACK):
+            sum_halves(2, t)
         take_root(2)
+        turn_inputs(2)
+        normalise(4)
+        make_feats(1)
         normalise(5)
+        group(2, HALF)
         turn(4, HALF)
-        add_bias(1)
-        make_feats(2)
         normalise(6)
-        group(4, HALF)
+        copy_inputs(2)
+        round_feats(0)
         invert(2)
         normalise(7)
         make_r(2)
-        turn(6, HALF)
         spread(2)
+        round_feats(1)
+        turn(6, HALF)
+        make_feats(2)
+        group(4, HALF)
         quantise(0, PACK)
         group(6, HALF)
-        quantise_feats(0, 2)
-        add_bias(2)
         normalise(8)
-        multiply(0, PACK, False)
+        quantise_feats(0, 2)
         normalise(9)
         turn(8, HALF)
-        quantise(PACK, PACK)
-        group(8, HALF)
+        round_feats(2)
         normalise(10)
-        multiply(PACK, PACK, False)
+        group(8, HALF)
+        multiply(0, PACK, False)
         turn(10, 1)
+        quantise(PACK, PACK)
         normalise(11)
+        multiply(PACK, PACK, False)
         group(10, 1)
         turn(11, 1)
         quantise_feats(2, 1)

@@ -24,6 +24,9 @@ FLOPS = 2 * GRAPHS * NODES * (NODES * DIM + FEATS * DIM)
 
 UNITS = GRAPHS * PACK
 HALF = 2
+IDLE_N = 256
+HEAD_PASSES = 14
+LATER_PASSES = 2
 
 
 def tile_gcn_s_kernel(tc, inputs, adj, W_kernel, W_bias, out):
@@ -65,8 +68,15 @@ def tile_gcn_s_kernel(tc, inputs, adj, W_kernel, W_bias, out):
         nc.sync.dma_start(out=w_sb[:], in_=W_kernel)
         load_adj(2, HALF)
 
+        idle_grouped = const.tile([P, IDLE_N * PACK], BF16, align_bytes=64)
+        nc.vector.memset(idle_grouped[:].bitcast(U32), 0x3F803F80)
         one = const.tile([P, 1], F32)
         nc.vector.memset(one[:], 1.0)
+        idle_codes = const.tile([P, IDLE_N], U32, align_bytes=64)
+        idle_scales = const.tile([P, IDLE_N], U8, align_bytes=64)
+        nc.vector.quantize_mx(
+            out=idle_codes[:].bitcast(FP8X4), scales=idle_scales[:], in_=idle_grouped[:]
+        )
         warm = const.tile([P, 1], F32)
         nc.scalar.activation(out=warm[:], in_=one[:], func=FUNC.Sqrt)
         ones = const.tile([P, 1], BF16)
@@ -78,6 +88,17 @@ def tile_gcn_s_kernel(tc, inputs, adj, W_kernel, W_bias, out):
 
         def bank(dtype):
             return psum.tile([P, PACK, P], dtype, name="bank", tag="bank", bufs=4)
+
+        idle_ps = bank(F32)
+
+        def keep_busy(passes):
+            for i in range(passes):
+                nc.tensor.matmul_mx(
+                    out=idle_ps[:, 0:HALF, :].rearrange("p t q -> p (t q)"),
+                    lhsT=idle_codes[:, 0:P].bitcast(FP8X4), lhsT_scale=idle_scales[:, 0:P],
+                    rhs=idle_codes[:].bitcast(FP8X4), rhs_scale=idle_scales[:],
+                    start=True, stop=True,
+                )
 
         degree_tiles = []
         root_tiles = []
@@ -279,7 +300,9 @@ def tile_gcn_s_kernel(tc, inputs, adj, W_kernel, W_bias, out):
         take_root(0)
         invert(0)
         make_r(0)
+        keep_busy(HEAD_PASSES)
         spread(0)
+        keep_busy(LATER_PASSES)
         sum_by_scalar(1, 0)
         sum_by_vector(1, 1)
         sum_by_scalar(1, 2)

@@ -24,9 +24,8 @@ FLOPS = 2 * GRAPHS * NODES * (NODES * DIM + FEATS * DIM)
 
 UNITS = GRAPHS * PACK
 HALF = 2
-IDLE_N = 256
-HEAD_PASSES = 14
-LATER_PASSES = 2
+HEAD_PASSES = 28
+LATER_PASSES = 8
 
 
 def tile_gcn_s_kernel(tc, inputs, adj, W_kernel, W_bias, out):
@@ -68,12 +67,12 @@ def tile_gcn_s_kernel(tc, inputs, adj, W_kernel, W_bias, out):
         nc.sync.dma_start(out=w_sb[:], in_=W_kernel)
         load_adj(2, HALF)
 
-        idle_grouped = const.tile([P, IDLE_N * PACK], BF16, align_bytes=64)
+        idle_grouped = const.tile([P, P * PACK], BF16, align_bytes=64)
         nc.vector.memset(idle_grouped[:].bitcast(U32), 0x3F803F80)
         one = const.tile([P, 1], F32)
         nc.vector.memset(one[:], 1.0)
-        idle_codes = const.tile([P, IDLE_N], U32, align_bytes=64)
-        idle_scales = const.tile([P, IDLE_N], U8, align_bytes=64)
+        idle_codes = const.tile([P, P], U32, align_bytes=64)
+        idle_scales = const.tile([P, P], U8, align_bytes=64)
         nc.vector.quantize_mx(
             out=idle_codes[:].bitcast(FP8X4), scales=idle_scales[:], in_=idle_grouped[:]
         )
@@ -89,13 +88,11 @@ def tile_gcn_s_kernel(tc, inputs, adj, W_kernel, W_bias, out):
         def bank(dtype):
             return psum.tile([P, PACK, P], dtype, name="bank", tag="bank", bufs=4)
 
-        idle_ps = bank(F32)
-
-        def keep_busy(passes):
+        def keep_busy(target, passes):
             for i in range(passes):
                 nc.tensor.matmul_mx(
-                    out=idle_ps[:, 0:HALF, :].rearrange("p t q -> p (t q)"),
-                    lhsT=idle_codes[:, 0:P].bitcast(FP8X4), lhsT_scale=idle_scales[:, 0:P],
+                    out=target[:, i % PACK, :],
+                    lhsT=idle_codes[:].bitcast(FP8X4), lhsT_scale=idle_scales[:],
                     rhs=idle_codes[:].bitcast(FP8X4), rhs_scale=idle_scales[:],
                     start=True, stop=True,
                 )
@@ -160,13 +157,17 @@ def tile_gcn_s_kernel(tc, inputs, adj, W_kernel, W_bias, out):
 
         spread_banks = []
 
-        def spread(b):
+        def open_spread(passes):
             r_ps = psum.tile([P, PACK, P], F32, name="r_ps", bufs=2)
+            keep_busy(r_ps, passes)
+            spread_banks.append(r_ps)
+
+        def spread(b):
             for t in range(PACK):
                 nc.tensor.transpose(
-                    r_ps[:, t, :], r_tiles[b][:, t : t + 1].to_broadcast([P, P]), ident_f32[:]
+                    spread_banks[b][:, t, :], r_tiles[b][:, t : t + 1].to_broadcast([P, P]),
+                    ident_f32[:],
                 )
-            spread_banks.append(r_ps)
 
         xT_banks = {}
         xT_tiles = {}
@@ -268,9 +269,10 @@ def tile_gcn_s_kernel(tc, inputs, adj, W_kernel, W_bias, out):
                 in_=grouped_tiles[b][:, tiles, :, :].rearrange("c t n j -> c (t n j)"),
             )
 
-        def multiply(first_unit, count, by_vector):
+        def multiply(first_unit, count, by_vector, passes=0):
             b, t0 = divmod(first_unit, PACK)
             out_ps = bank(F32)
+            keep_busy(out_ps, passes)
             for h in range(count):
                 nc.tensor.matmul_mx(
                     out=out_ps[:, h, :],
@@ -300,9 +302,9 @@ def tile_gcn_s_kernel(tc, inputs, adj, W_kernel, W_bias, out):
         take_root(0)
         invert(0)
         make_r(0)
-        keep_busy(HEAD_PASSES)
+        open_spread(HEAD_PASSES)
         spread(0)
-        keep_busy(LATER_PASSES)
+        open_spread(LATER_PASSES)
         sum_by_scalar(1, 0)
         sum_by_vector(1, 1)
         sum_by_scalar(1, 2)
@@ -341,6 +343,7 @@ def tile_gcn_s_kernel(tc, inputs, adj, W_kernel, W_bias, out):
         normalise(5)
         group(2, HALF)
         turn(4, HALF)
+        open_spread(LATER_PASSES)
         normalise(6)
         copy_inputs(2)
         round_feats(0)
@@ -361,7 +364,7 @@ def tile_gcn_s_kernel(tc, inputs, adj, W_kernel, W_bias, out):
         round_feats(2)
         normalise(10)
         group(8, HALF)
-        multiply(0, PACK, False)
+        multiply(0, PACK, False, LATER_PASSES // 2)
         turn(10, 1)
         quantise(PACK, PACK)
         normalise(11)

@@ -62,10 +62,11 @@ def tile_gcn_s_kernel(tc, inputs, adj, W_kernel, W_bias, out):
         load_adj(0, 1)
         load_adj(1, HALF)
         nc.sync.dma_start(out=bias_row[0:1, :], in_=W_bias.rearrange("(o d) -> o d", o=1))
-        for b in range(GRAPHS):
-            load_inputs(b)
-        nc.sync.dma_start(out=w_sb[:], in_=W_kernel)
+        load_inputs(0)
+        load_inputs(1)
         load_adj(2, HALF)
+        nc.sync.dma_start(out=w_sb[:], in_=W_kernel)
+        load_inputs(2)
 
         idle_grouped = const.tile([P, P * PACK], BF16, align_bytes=64)
         nc.vector.memset(idle_grouped[:].bitcast(U32), 0x3F803F80)
@@ -193,11 +194,12 @@ def tile_gcn_s_kernel(tc, inputs, adj, W_kernel, W_bias, out):
             for j in range(PACK):
                 nc.tensor.matmul(
                     out=feats_ps[:, j, :], lhsT=bias_col[:].to_broadcast([P, P]), rhs=ident_f32[:],
-                    is_transpose=True, start=True, stop=False,
+                    is_transpose=True, start=j == 0, stop=False,
                 )
+            for j in range(PACK):
                 nc.tensor.matmul(
                     out=feats_ps[:, j, :], lhsT=xT_tiles[b][:, j, :], rhs=w_sb[:],
-                    start=False, stop=True,
+                    start=False, stop=j == PACK - 1,
                 )
             feats_banks[b] = feats_ps
 
@@ -269,7 +271,9 @@ def tile_gcn_s_kernel(tc, inputs, adj, W_kernel, W_bias, out):
                 in_=grouped_tiles[b][:, tiles, :, :].rearrange("c t n j -> c (t n j)"),
             )
 
-        def multiply(first_unit, count, by_vector, passes=0):
+        out_banks = {}
+
+        def multiply(first_unit, count, passes=0):
             b, t0 = divmod(first_unit, PACK)
             out_ps = bank(F32)
             keep_busy(out_ps, passes)
@@ -283,6 +287,11 @@ def tile_gcn_s_kernel(tc, inputs, adj, W_kernel, W_bias, out):
                     start=True,
                     stop=True,
                 )
+            out_banks[first_unit] = out_ps
+
+        def store(first_unit, count, by_vector=False):
+            b, t0 = divmod(first_unit, PACK)
+            out_ps = out_banks[first_unit]
             out_sb = work.tile([P, PACK, DIM], F32, name="out_sb", bufs=5)
             if by_vector:
                 nc.vector.tensor_scalar_max(
@@ -304,20 +313,20 @@ def tile_gcn_s_kernel(tc, inputs, adj, W_kernel, W_bias, out):
         make_r(0)
         open_spread(HEAD_PASSES)
         spread(0)
-        open_spread(LATER_PASSES)
-        sum_by_scalar(1, 0)
-        sum_by_vector(1, 1)
-        sum_by_scalar(1, 2)
-        sum_by_vector(1, 3)
         bias_ps = bank(F32)
         nc.tensor.matmul(
             out=bias_ps[:, 0, 0:1], lhsT=bias_row[:], rhs=ones[:], start=True, stop=True
         )
+        sum_by_scalar(1, 0)
+        sum_by_vector(1, 1)
+        sum_by_scalar(1, 2)
+        sum_by_vector(1, 3)
+        take_root(1)
         bias_col = const.tile([P, 1], F32)
         nc.scalar.copy(out=bias_col[:], in_=bias_ps[:, 0, 0:1])
-        take_root(1)
         turn_inputs(0)
         turn_inputs(1)
+        open_spread(LATER_PASSES)
         for t in range(PACK):
             add_halves(2, t)
         normalise(0)
@@ -348,9 +357,9 @@ def tile_gcn_s_kernel(tc, inputs, adj, W_kernel, W_bias, out):
         copy_inputs(2)
         round_feats(0)
         invert(2)
-        normalise(7)
         make_r(2)
         spread(2)
+        normalise(7)
         round_feats(1)
         turn(6, HALF)
         make_feats(2)
@@ -364,17 +373,23 @@ def tile_gcn_s_kernel(tc, inputs, adj, W_kernel, W_bias, out):
         round_feats(2)
         normalise(10)
         group(8, HALF)
-        multiply(0, PACK, False, LATER_PASSES // 2)
+        multiply(0, PACK, LATER_PASSES // 2)
+        store(0, PACK)
         turn(10, 1)
         quantise(PACK, PACK)
         normalise(11)
-        multiply(PACK, PACK, False)
-        group(10, 1)
+        group(10, 1, True)
+        multiply(PACK, PACK)
         turn(11, 1)
+        store(PACK, PACK)
         quantise_feats(2, 1)
         quantise(8, HALF)
-        group(11, 1, True)
-        multiply(8, HALF, False)
-        quantise(10, HALF)
-        multiply(10, 1, False)
-        multiply(11, 1, True)
+        multiply(8, HALF)
+        group(11, 1)
+        quantise(10, 1)
+        multiply(10, 1)
+        store(8, HALF)
+        quantise(11, 1)
+        multiply(11, 1)
+        store(10, 1)
+        store(11, 1, True)

@@ -138,23 +138,29 @@ def tile_gcn_s_kernel(tc, inputs, adj, W_kernel, W_bias, out):
                 accum_out=degree_tiles[b][:, t : t + 1],
             )
 
-        def take_root(b):
+        for b in range(GRAPHS):
             root = graph.tile([P, PACK], F32, name="root")
-            nc.scalar.activation(out=root[:], in_=degree_tiles[b][:], func=FUNC.Sqrt)
             root_tiles.append(root)
-
-        def invert(b):
             inverse = graph.tile([P, PACK], F32, name="inverse")
-            nc.vector.reciprocal(out=inverse[:], in_=degree_tiles[b][:])
             inverse_tiles.append(inverse)
-
-        def make_r(b):
             r = graph.tile([P, PACK], F32, name="r")
-            nc.vector.scalar_tensor_tensor(
-                out=r[:], in0=inverse_tiles[b][:], scalar=HUGE, in1=root_tiles[b][:],
-                op0=ALU.min, op1=ALU.mult,
-            )
             r_tiles.append(r)
+
+        def take_root(b, first=0, end=PACK):
+            nc.scalar.activation(
+                out=root_tiles[b][:, first:end], in_=degree_tiles[b][:, first:end], func=FUNC.Sqrt
+            )
+
+        def invert(b, first=0, end=PACK):
+            nc.vector.reciprocal(
+                out=inverse_tiles[b][:, first:end], in_=degree_tiles[b][:, first:end]
+            )
+
+        def make_r(b, first=0, end=PACK):
+            nc.vector.scalar_tensor_tensor(
+                out=r_tiles[b][:, first:end], in0=inverse_tiles[b][:, first:end], scalar=HUGE,
+                in1=root_tiles[b][:, first:end], op0=ALU.min, op1=ALU.mult,
+            )
 
         spread_banks = []
 
@@ -163,8 +169,8 @@ def tile_gcn_s_kernel(tc, inputs, adj, W_kernel, W_bias, out):
             keep_busy(r_ps, passes)
             spread_banks.append(r_ps)
 
-        def spread(b):
-            for t in range(PACK):
+        def spread(b, first=0, end=PACK):
+            for t in range(first, end):
                 nc.tensor.transpose(
                     spread_banks[b][:, t, :], r_tiles[b][:, t : t + 1].to_broadcast([P, P]),
                     ident_f32[:],
@@ -189,8 +195,9 @@ def tile_gcn_s_kernel(tc, inputs, adj, W_kernel, W_bias, out):
             nc.scalar.copy(out=xT_sb[:], in_=xT_banks[b][:])
             xT_tiles[b] = xT_sb
 
-        def make_feats(b):
+        def make_feats(b, passes=0):
             feats_ps = bank(F32)
+            keep_busy(feats_ps, passes)
             for j in range(PACK):
                 nc.tensor.matmul(
                     out=feats_ps[:, j, :], lhsT=bias_col[:].to_broadcast([P, P]), rhs=ident_f32[:],
@@ -307,11 +314,14 @@ def tile_gcn_s_kernel(tc, inputs, adj, W_kernel, W_bias, out):
         sum_by_vector(0, 0)
         sum_by_scalar(0, 1)
         sum_by_vector(0, 2)
-        sum_by_vector(0, 3)
-        take_root(0)
-        invert(0)
-        make_r(0)
         open_spread(HEAD_PASSES)
+        take_root(0, 0, PACK - 1)
+        sum_by_vector(0, 3)
+        take_root(0, PACK - 1, PACK)
+        invert(0, 0, PACK - 1)
+        invert(0, PACK - 1, PACK)
+        make_r(0, 0, PACK - 1)
+        make_r(0, PACK - 1, PACK)
         spread(0)
         bias_ps = bank(F32)
         nc.tensor.matmul(
@@ -351,18 +361,18 @@ def tile_gcn_s_kernel(tc, inputs, adj, W_kernel, W_bias, out):
         make_feats(1)
         normalise(5)
         group(2, HALF)
-        turn(4, HALF)
-        open_spread(LATER_PASSES)
+        open_spread(LATER_PASSES // 2)
         normalise(6)
         copy_inputs(2)
         round_feats(0)
         invert(2)
         make_r(2)
         spread(2)
+        turn(4, HALF)
         normalise(7)
         round_feats(1)
         turn(6, HALF)
-        make_feats(2)
+        make_feats(2, LATER_PASSES // 2)
         group(4, HALF)
         quantise(0, PACK)
         group(6, HALF)
@@ -376,20 +386,20 @@ def tile_gcn_s_kernel(tc, inputs, adj, W_kernel, W_bias, out):
         multiply(0, PACK, LATER_PASSES // 2)
         store(0, PACK)
         turn(10, 1)
+        group(10, 1)
         quantise(PACK, PACK)
         normalise(11)
-        group(10, 1, True)
         multiply(PACK, PACK)
         turn(11, 1)
-        store(PACK, PACK)
+        group(11, 1)
         quantise_feats(2, 1)
         quantise(8, HALF)
+        store(PACK, PACK, True)
         multiply(8, HALF)
-        group(11, 1)
-        quantise(10, 1)
-        multiply(10, 1)
         store(8, HALF)
+        quantise(10, 1)
         quantise(11, 1)
+        multiply(10, 1)
         multiply(11, 1)
         store(10, 1)
         store(11, 1, True)

@@ -337,7 +337,7 @@ def tile_gcn_s_kernel(tc, inputs, adj, W_kernel, W_bias, out):
         turn_inputs(0)
         turn_inputs(1)
         open_spread(LATER_PASSES)
-        for t in range(PACK):
+        for t in range(HALF, PACK):
             add_halves(2, t)
         normalise(0)
         copy_inputs(0)
@@ -349,11 +349,12 @@ def tile_gcn_s_kernel(tc, inputs, adj, W_kernel, W_bias, out):
         spread(1)
         make_feats(0)
         normalise(2)
-        sum_halves(2, 0)
+        sum_by_scalar(2, 0)
+        sum_by_scalar(2, 1)
         group(0, HALF)
         normalise(3)
         turn(2, HALF)
-        for t in range(1, PACK):
+        for t in range(HALF, PACK):
             sum_halves(2, t)
         take_root(2)
         turn_inputs(2)

@@ -24,7 +24,7 @@ FLOPS = 2 * GRAPHS * NODES * (NODES * DIM + FEATS * DIM)
 
 UNITS = GRAPHS * PACK
 HALF = 2
-HEAD_PASSES = 28
+HEAD_PASSES = 36
 LATER_PASSES = 8
 
 
@@ -40,6 +40,8 @@ def tile_gcn_s_kernel(tc, inputs, adj, W_kernel, W_bias, out):
         w_sb = const.tile([FEATS, DIM], BF16)
         bias_row = const.tile([P, DIM], BF16)
         x_sb = const.tile([P, GRAPHS, HALF, PAIR, FEATS], BF16)
+        idle_grouped = const.tile([P, P * PACK], BF16, align_bytes=64)
+        nc.gpsimd.memset(idle_grouped[:].bitcast(U32), 0x3F803F80)
         nc.gpsimd.memset(bias_row[:], 0.0)
         adj_tiles = []
         for b in range(GRAPHS):
@@ -68,15 +70,13 @@ def tile_gcn_s_kernel(tc, inputs, adj, W_kernel, W_bias, out):
         nc.sync.dma_start(out=w_sb[:], in_=W_kernel)
         load_inputs(2)
 
-        idle_grouped = const.tile([P, P * PACK], BF16, align_bytes=64)
-        nc.vector.memset(idle_grouped[:].bitcast(U32), 0x3F803F80)
-        one = const.tile([P, 1], F32)
-        nc.vector.memset(one[:], 1.0)
         idle_codes = const.tile([P, P], U32, align_bytes=64)
         idle_scales = const.tile([P, P], U8, align_bytes=64)
         nc.vector.quantize_mx(
             out=idle_codes[:].bitcast(FP8X4), scales=idle_scales[:], in_=idle_grouped[:]
         )
+        one = const.tile([P, 1], F32)
+        nc.vector.memset(one[:], 1.0)
         warm = const.tile([P, 1], F32)
         nc.scalar.activation(out=warm[:], in_=one[:], func=FUNC.Sqrt)
         ones = const.tile([P, 1], BF16)
@@ -195,9 +195,8 @@ def tile_gcn_s_kernel(tc, inputs, adj, W_kernel, W_bias, out):
             nc.scalar.copy(out=xT_sb[:], in_=xT_banks[b][:])
             xT_tiles[b] = xT_sb
 
-        def make_feats(b, passes=0):
+        def make_feats(b):
             feats_ps = bank(F32)
-            keep_busy(feats_ps, passes)
             for j in range(PACK):
                 nc.tensor.matmul(
                     out=feats_ps[:, j, :], lhsT=bias_col[:].to_broadcast([P, P]), rhs=ident_f32[:],
@@ -242,15 +241,21 @@ def tile_gcn_s_kernel(tc, inputs, adj, W_kernel, W_bias, out):
             )
             norm_tiles[unit] = norm
 
-        def turn(first_unit, count):
+        def open_words(first_unit, passes):
             word_ps = psum.tile([P, HALF, HALF, P], F32, name="word_ps", bufs=2)
+            keep_busy(word_ps[:].rearrange("c h u n -> c (h u) n"), passes)
+            word_banks[first_unit] = word_ps
+
+        def turn(first_unit, count):
+            if first_unit not in word_banks:
+                open_words(first_unit, 0)
             for h in range(count):
                 words = norm_tiles[first_unit + h][:].bitcast(F32)
                 for u in range(HALF):
                     nc.tensor.transpose(
-                        word_ps[:, h, u, :], words[:, u * P : (u + 1) * P], ident_f32[:]
+                        word_banks[first_unit][:, h, u, :], words[:, u * P : (u + 1) * P],
+                        ident_f32[:],
                     )
-            word_banks[first_unit] = word_ps
 
         def group(first_unit, count, by_vector=False):
             b, t0 = divmod(first_unit, PACK)
@@ -280,10 +285,16 @@ def tile_gcn_s_kernel(tc, inputs, adj, W_kernel, W_bias, out):
 
         out_banks = {}
 
-        def multiply(first_unit, count, passes=0):
-            b, t0 = divmod(first_unit, PACK)
+        def open_out(first_unit, passes):
             out_ps = bank(F32)
             keep_busy(out_ps, passes)
+            out_banks[first_unit] = out_ps
+
+        def multiply(first_unit, count):
+            b, t0 = divmod(first_unit, PACK)
+            if first_unit not in out_banks:
+                open_out(first_unit, 0)
+            out_ps = out_banks[first_unit]
             for h in range(count):
                 nc.tensor.matmul_mx(
                     out=out_ps[:, h, :],
@@ -294,7 +305,6 @@ def tile_gcn_s_kernel(tc, inputs, adj, W_kernel, W_bias, out):
                     start=True,
                     stop=True,
                 )
-            out_banks[first_unit] = out_ps
 
         def store(first_unit, count, by_vector=False):
             b, t0 = divmod(first_unit, PACK)
@@ -362,7 +372,7 @@ def tile_gcn_s_kernel(tc, inputs, adj, W_kernel, W_bias, out):
         make_feats(1)
         normalise(5)
         group(2, HALF)
-        open_spread(LATER_PASSES // 2)
+        open_spread(LATER_PASSES)
         normalise(6)
         copy_inputs(2)
         round_feats(0)
@@ -373,7 +383,8 @@ def tile_gcn_s_kernel(tc, inputs, adj, W_kernel, W_bias, out):
         normalise(7)
         round_feats(1)
         turn(6, HALF)
-        make_feats(2, LATER_PASSES // 2)
+        make_feats(2)
+        open_out(0, LATER_PASSES // 2)
         group(4, HALF)
         quantise(0, PACK)
         group(6, HALF)
@@ -384,7 +395,7 @@ def tile_gcn_s_kernel(tc, inputs, adj, W_kernel, W_bias, out):
         round_feats(2)
         normalise(10)
         group(8, HALF)
-        multiply(0, PACK, LATER_PASSES // 2)
+        multiply(0, PACK)
         store(0, PACK)
         turn(10, 1)
         group(10, 1)

@@ -24,7 +24,7 @@ FLOPS = 2 * GRAPHS * NODES * (NODES * DIM + FEATS * DIM)
 
 UNITS = GRAPHS * PACK
 HALF = 2
-HEAD_PASSES = 36
+HEAD_PASSES = 30
 LATER_PASSES = 8
 
 

from contextlib import ExitStack

import concourse.mybir as mybir
from concourse.masks import make_identity

BF16 = mybir.dt.bfloat16
F32 = mybir.dt.float32
U32 = mybir.dt.uint32
U8 = mybir.dt.uint8
FP8X4 = mybir.dt.float8_e4m3fn_x4
ALU = mybir.AluOpType
FUNC = mybir.ActivationFunctionType

GRAPHS = 3
NODES = 512
FEATS = 128
DIM = 128
P = 128
PACK = 4
PAIR = 2
HUGE = 3.0e38

FLOPS = 2 * GRAPHS * NODES * (NODES * DIM + FEATS * DIM)

UNITS = GRAPHS * PACK
HALF = 2
HEAD_PASSES = 30
LATER_PASSES = 8


def tile_gcn_s_kernel(tc, inputs, adj, W_kernel, W_bias, out):
    nc = tc.nc
    with ExitStack() as stack:
        const = stack.enter_context(tc.tile_pool(name="const", bufs=1))
        graph = stack.enter_context(tc.tile_pool(name="graph", bufs=GRAPHS))
        work = stack.enter_context(tc.tile_pool(name="work", bufs=2))
        psum = stack.enter_context(tc.psum_pool(name="psum", bufs=1))
        stack.enter_context(tc.manual_schedule())

        w_sb = const.tile([FEATS, DIM], BF16)
        bias_row = const.tile([P, DIM], BF16)
        x_sb = const.tile([P, GRAPHS, HALF, PAIR, FEATS], BF16)
        idle_grouped = const.tile([P, P * PACK], BF16, align_bytes=64)
        nc.gpsimd.memset(idle_grouped[:].bitcast(U32), 0x3F803F80)
        nc.gpsimd.memset(bias_row[:], 0.0)
        adj_tiles = []
        for b in range(GRAPHS):
            adj_sb = graph.tile([P, PACK, NODES], BF16)
            adj_tiles.append(adj_sb)

        def load_adj(b, size):
            adj_rows = adj[b].rearrange("(p t) m -> p t m", t=PACK)
            for t in range(0, PACK, size):
                nc.sync.dma_start(
                    out=adj_tiles[b][:, t : t + size, :], in_=adj_rows[:, t : t + size, :]
                )

        def load_inputs(b):
            nc.sync.dma_start(
                out=x_sb[:, b, :, :, :],
                in_=inputs[b].rearrange("(u c e) f -> c u e f", u=HALF, e=PAIR),
            )

        load_adj(0, 1)
        load_adj(1, HALF)
        nc.sync.dma_start(out=bias_row[0:1, :], in_=W_bias.rearrange("(o d) -> o d", o=1))
        load_inputs(0)
        load_inputs(1)
        load_adj(2, HALF)
        nc.sync.dma_start(out=w_sb[:], in_=W_kernel)
        load_inputs(2)

        idle_codes = const.tile([P, P], U32, align_bytes=64)
        idle_scales = const.tile([P, P], U8, align_bytes=64)
        nc.vector.quantize_mx(
            out=idle_codes[:].bitcast(FP8X4), scales=idle_scales[:], in_=idle_grouped[:]
        )
        one = const.tile([P, 1], F32)
        nc.vector.memset(one[:], 1.0)
        warm = const.tile([P, 1], F32)
        nc.scalar.activation(out=warm[:], in_=one[:], func=FUNC.Sqrt)
        ones = const.tile([P, 1], BF16)
        nc.gpsimd.memset(ones[:], 1.0)
        ident_bf = const.tile([P, P], BF16)
        make_identity(nc, ident_bf[:])
        ident_f32 = const.tile([P, P], F32)
        make_identity(nc, ident_f32[:])

        def bank(dtype):
            return psum.tile([P, PACK, P], dtype, name="bank", tag="bank", bufs=4)

        def keep_busy(target, passes):
            for i in range(passes):
                nc.tensor.matmul_mx(
                    out=target[:, i % PACK, :],
                    lhsT=idle_codes[:].bitcast(FP8X4), lhsT_scale=idle_scales[:],
                    rhs=idle_codes[:].bitcast(FP8X4), rhs_scale=idle_scales[:],
                    start=True, stop=True,
                )

        degree_tiles = []
        root_tiles = []
        inverse_tiles = []
        r_tiles = []
        for b in range(GRAPHS):
            degree = graph.tile([P, PACK], F32, name="degree")
            degree_tiles.append(degree)

        def sum_by_scalar(b, t):
            unused = work.tile([P, NODES], BF16, name="unused_s")
            nc.scalar.activation(
                out=unused[:], in_=adj_tiles[b][:, t, :], func=FUNC.Copy,
                accum_out=degree_tiles[b][:, t : t + 1],
            )

        def sum_by_vector(b, t):
            unused = work.tile([P, NODES], BF16, name="unused_v")
            nc.vector.tensor_scalar(
                out=unused[:], in0=adj_tiles[b][:, t, :], scalar1=1.0, scalar2=None,
                op0=ALU.mult, op1=ALU.add, accum_out=degree_tiles[b][:, t : t + 1],
            )

        half_sums = {}

        def add_halves(b, t):
            rows = adj_tiles[b][:, t, :]
            half_sum = work.tile([P, NODES // 2], F32, name="half_sum", bufs=4)
            nc.gpsimd.tensor_tensor(
                out=half_sum[:], in0=rows[:, 0 : NODES // 2], in1=rows[:, NODES // 2 : NODES],
                op=ALU.add,
            )
            half_sums[b, t] = half_sum

        def sum_halves(b, t):
            unused = work.tile([P, NODES // 2], F32, name="unused_h")
            nc.scalar.activation(
                out=unused[:], in_=half_sums[b, t][:], func=FUNC.Copy,
                accum_out=degree_tiles[b][:, t : t + 1],
            )

        for b in range(GRAPHS):
            root = graph.tile([P, PACK], F32, name="root")
            root_tiles.append(root)
            inverse = graph.tile([P, PACK], F32, name="inverse")
            inverse_tiles.append(inverse)
            r = graph.tile([P, PACK], F32, name="r")
            r_tiles.append(r)

        def take_root(b, first=0, end=PACK):
            nc.scalar.activation(
                out=root_tiles[b][:, first:end], in_=degree_tiles[b][:, first:end], func=FUNC.Sqrt
            )

        def invert(b, first=0, end=PACK):
            nc.vector.reciprocal(
                out=inverse_tiles[b][:, first:end], in_=degree_tiles[b][:, first:end]
            )

        def make_r(b, first=0, end=PACK):
            nc.vector.scalar_tensor_tensor(
                out=r_tiles[b][:, first:end], in0=inverse_tiles[b][:, first:end], scalar=HUGE,
                in1=root_tiles[b][:, first:end], op0=ALU.min, op1=ALU.mult,
            )

        spread_banks = []

        def open_spread(passes):
            r_ps = psum.tile([P, PACK, P], F32, name="r_ps", bufs=2)
            keep_busy(r_ps, passes)
            spread_banks.append(r_ps)

        def spread(b, first=0, end=PACK):
            for t in range(first, end):
                nc.tensor.transpose(
                    spread_banks[b][:, t, :], r_tiles[b][:, t : t + 1].to_broadcast([P, P]),
                    ident_f32[:],
                )

        xT_banks = {}
        xT_tiles = {}
        feats_banks = {}
        feats_grouped = const.tile([P, GRAPHS, DIM, PACK], BF16, align_bytes=64)
        feats_codes = const.tile([P, GRAPHS, DIM], U32, align_bytes=64)
        feats_scales = const.tile([P, GRAPHS, DIM], U8, align_bytes=64)

        def turn_inputs(b):
            xT_ps = bank(BF16)
            for j in range(PACK):
                u, e = divmod(j, PAIR)
                nc.tensor.transpose(xT_ps[:, j, :], x_sb[:, b, u, e, :], ident_bf[:])
            xT_banks[b] = xT_ps

        def copy_inputs(b):
            xT_sb = graph.tile([FEATS, PACK, P], BF16, name="xT_sb")
            nc.scalar.copy(out=xT_sb[:], in_=xT_banks[b][:])
            xT_tiles[b] = xT_sb

        def make_feats(b):
            feats_ps = bank(F32)
            for j in range(PACK):
                nc.tensor.matmul(
                    out=feats_ps[:, j, :], lhsT=bias_col[:].to_broadcast([P, P]), rhs=ident_f32[:],
                    is_transpose=True, start=j == 0, stop=False,
                )
            for j in range(PACK):
                nc.tensor.matmul(
                    out=feats_ps[:, j, :], lhsT=xT_tiles[b][:, j, :], rhs=w_sb[:],
                    start=False, stop=j == PACK - 1,
                )
            feats_banks[b] = feats_ps

        def round_feats(b):
            nc.scalar.copy(
                out=feats_grouped[:, b, :, :], in_=feats_banks[b][:].rearrange("c j d -> c d j")
            )

        def quantise_feats(first, count):
            graphs = slice(first, first + count)
            nc.vector.quantize_mx(
                out=feats_codes[:, graphs, :].rearrange("c b d -> c (b d)").bitcast(FP8X4),
                scales=feats_scales[:, graphs, :].rearrange("c b d -> c (b d)"),
                in_=feats_grouped[:, graphs, :, :].rearrange("c b d j -> c (b d j)"),
            )

        norm_tiles = {}
        word_banks = {}
        grouped_tiles = []
        codes_tiles = []
        scales_tiles = []

        def normalise(unit):
            b, t = divmod(unit, PACK)
            norm = work.tile([P, NODES], BF16, name="norm", bufs=4)
            split = "p (q t) -> p q t"
            nc.vector.scalar_tensor_tensor(
                out=norm[:].rearrange(split, t=PACK),
                in0=adj_tiles[b][:, t, :].rearrange(split, t=PACK),
                scalar=r_tiles[b][:, t : t + 1],
                in1=spread_banks[b][:].rearrange("p t q -> p q t"),
                op0=ALU.mult, op1=ALU.mult,
            )
            norm_tiles[unit] = norm

        def open_words(first_unit, passes):
            word_ps = psum.tile([P, HALF, HALF, P], F32, name="word_ps", bufs=2)
            keep_busy(word_ps[:].rearrange("c h u n -> c (h u) n"), passes)
            word_banks[first_unit] = word_ps

        def turn(first_unit, count):
            if first_unit not in word_banks:
                open_words(first_unit, 0)
            for h in range(count):
                words = norm_tiles[first_unit + h][:].bitcast(F32)
                for u in range(HALF):
                    nc.tensor.transpose(
                        word_banks[first_unit][:, h, u, :], words[:, u * P : (u + 1) * P],
                        ident_f32[:],
                    )

        def group(first_unit, count, by_vector=False):
            b, t0 = divmod(first_unit, PACK)
            if t0 == 0:
                norm_grouped = graph.tile([P, PACK, P, PACK], BF16, align_bytes=64)
                grouped_tiles.append(norm_grouped)
                norm_codes = graph.tile([P, PACK, P], U32, align_bytes=64)
                codes_tiles.append(norm_codes)
                norm_scales = graph.tile([P, PACK, P], U8, align_bytes=64)
                scales_tiles.append(norm_scales)
            copy = nc.vector.tensor_copy if by_vector else nc.scalar.copy
            copy(
                out=grouped_tiles[b][:, t0 : t0 + count, :, :]
                .rearrange("c t n j -> c (t n j)").bitcast(F32)
                .rearrange("c (t n u) -> c t n u", n=P, u=HALF),
                in_=word_banks[first_unit][:, 0:count, :, :].rearrange("c t u n -> c t n u"),
            )

        def quantise(first_unit, count):
            b, t0 = divmod(first_unit, PACK)
            tiles = slice(t0, t0 + count)
            nc.vector.quantize_mx(
                out=codes_tiles[b][:, tiles, :].rearrange("c t n -> c (t n)").bitcast(FP8X4),
                scales=scales_tiles[b][:, tiles, :].rearrange("c t n -> c (t n)"),
                in_=grouped_tiles[b][:, tiles, :, :].rearrange("c t n j -> c (t n j)"),
            )

        out_banks = {}

        def open_out(first_unit, passes):
            out_ps = bank(F32)
            keep_busy(out_ps, passes)
            out_banks[first_unit] = out_ps

        def multiply(first_unit, count):
            b, t0 = divmod(first_unit, PACK)
            if first_unit not in out_banks:
                open_out(first_unit, 0)
            out_ps = out_banks[first_unit]
            for h in range(count):
                nc.tensor.matmul_mx(
                    out=out_ps[:, h, :],
                    lhsT=codes_tiles[b][:, t0 + h, :].bitcast(FP8X4),
                    lhsT_scale=scales_tiles[b][:, t0 + h, :],
                    rhs=feats_codes[:, b, :].bitcast(FP8X4),
                    rhs_scale=feats_scales[:, b, :],
                    start=True,
                    stop=True,
                )

        def store(first_unit, count, by_vector=False):
            b, t0 = divmod(first_unit, PACK)
            out_ps = out_banks[first_unit]
            out_sb = work.tile([P, PACK, DIM], F32, name="out_sb", bufs=5)
            if by_vector:
                nc.vector.tensor_scalar_max(
                    out=out_sb[:, 0:count, :], in0=out_ps[:, 0:count, :], scalar1=0.0
                )
            else:
                nc.scalar.activation(
                    out=out_sb[:, 0:count, :], in_=out_ps[:, 0:count, :], func=FUNC.Relu
                )
            out_rows = out[b].rearrange("(p t) d -> p t d", t=PACK)
            nc.sync.dma_start(out=out_rows[:, t0 : t0 + count, :], in_=out_sb[:, 0:count, :])

        sum_by_vector(0, 0)
        sum_by_scalar(0, 1)
        sum_by_vector(0, 2)
        open_spread(HEAD_PASSES)
        take_root(0, 0, PACK - 1)
        sum_by_vector(0, 3)
        take_root(0, PACK - 1, PACK)
        invert(0, 0, PACK - 1)
        invert(0, PACK - 1, PACK)
        make_r(0, 0, PACK - 1)
        make_r(0, PACK - 1, PACK)
        spread(0)
        bias_ps = bank(F32)
        nc.tensor.matmul(
            out=bias_ps[:, 0, 0:1], lhsT=bias_row[:], rhs=ones[:], start=True, stop=True
        )
        sum_by_scalar(1, 0)
        sum_by_vector(1, 1)
        sum_by_scalar(1, 2)
        sum_by_vector(1, 3)
        take_root(1)
        bias_col = const.tile([P, 1], F32)
        nc.scalar.copy(out=bias_col[:], in_=bias_ps[:, 0, 0:1])
        turn_inputs(0)
        turn_inputs(1)
        open_spread(LATER_PASSES)
        for t in range(HALF, PACK):
            add_halves(2, t)
        normalise(0)
        copy_inputs(0)
        invert(1)
        normalise(1)
        copy_inputs(1)
        make_r(1)
        turn(0, HALF)
        spread(1)
        make_feats(0)
        normalise(2)
        sum_by_scalar(2, 0)
        sum_by_scalar(2, 1)
        group(0, HALF)
        normalise(3)
        turn(2, HALF)
        for t in range(HALF, PACK):
            sum_halves(2, t)
        take_root(2)
        turn_inputs(2)
        normalise(4)
        make_feats(1)
        normalise(5)
        group(2, HALF)
        open_spread(LATER_PASSES)
        normalise(6)
        copy_inputs(2)
        round_feats(0)
        invert(2)
        make_r(2)
        spread(2)
        turn(4, HALF)
        normalise(7)
        round_feats(1)
        turn(6, HALF)
        make_feats(2)
        open_out(0, LATER_PASSES // 2)
        group(4, HALF)
        quantise(0, PACK)
        group(6, HALF)
        normalise(8)
        quantise_feats(0, 2)
        normalise(9)
        turn(8, HALF)
        round_feats(2)
        normalise(10)
        group(8, HALF)
        multiply(0, PACK)
        store(0, PACK)
        turn(10, 1)
        group(10, 1)
        quantise(PACK, PACK)
        normalise(11)
        multiply(PACK, PACK)
        turn(11, 1)
        group(11, 1)
        quantise_feats(2, 1)
        quantise(8, HALF)
        store(PACK, PACK, True)
        multiply(8, HALF)
        store(8, HALF)
        quantise(10, 1)
        quantise(11, 1)
        multiply(10, 1)
        multiply(11, 1)
        store(10, 1)
        store(11, 1, True)
